import numpy as np
import ml_dtypes


def mxq(x, axis, fmt="e4m3"):
    dtype, down = {"e4m3": (ml_dtypes.float8_e4m3fn, 7), "e5m2": (ml_dtypes.float8_e5m2, 14)}[fmt]
    v = np.moveaxis(np.asarray(x, np.float32).astype(ml_dtypes.bfloat16).astype(np.float64), axis, -1)
    blocks = v.reshape(v.shape[:-1] + (-1, 32))
    amax = np.abs(blocks).max(-1, keepdims=True)
    byte = np.maximum(np.where(amax > 0, np.frexp(amax)[1] - 1 + 127, 0) - down, 1)
    scale = np.exp2(byte - 127.0)
    codes = (blocks / scale).astype(np.float32).astype(dtype).astype(np.float64)
    return np.moveaxis((codes * scale).reshape(v.shape), -1, axis)


WIDE = False


def mx_kscale(k):
    if not WIDE:
        return np.ones(k)
    levels = np.array([10, -10, 5, -5, 0])
    if k % 512:
        return np.exp2(np.random.permutation(np.resize(levels, k // 32))).repeat(32)
    a = np.empty((k // 512, 16))
    for p in range(k // 512):
        a[p, :8] = np.random.permutation(np.resize(levels, 8))
        for g in range(8):
            far = levels[np.abs(levels - a[p, g]) >= 10]
            a[p, g + 8] = far[np.random.randint(len(far))]
    return np.exp2(a.ravel()).repeat(32)


BF16 = ml_dtypes.bfloat16


def bf(x):
    return np.asarray(x, np.float32).astype(BF16)


def f64(x):
    return np.asarray(x).astype(np.float64)


B, D, U = 256, 2048, 2048
MASK_DENSITY = 1.0 / 16.0
W_STD = 1.0 / np.sqrt(U * MASK_DENSITY)


def setup_inputs():
    s, t = mx_kscale(U), mx_kscale(U)
    return {"h0": bf(np.random.standard_normal((B, U)) * s),
            "k1": bf(np.random.standard_normal((U, U)) * W_STD / s[:, None] * t),
            "k2": bf(np.random.standard_normal((U, U)) * W_STD / t[:, None]),
            "m1": bf(np.random.random((U, U)) < MASK_DENSITY),
            "m2": bf(np.random.random((U, U)) < MASK_DENSITY),
            "scaling": bf(np.random.uniform(1.25, 1.75, 1)),
            "bias": bf(np.random.standard_normal(U) * 0.5)}


def reference(h0, k1, k2, m1, m2, scaling, bias):
    w1 = f64(k1) * f64(m1)
    w2 = f64(k2) * f64(m2)
    h1 = mxq(f64(h0), 1, "e4m3") @ mxq(w1, 0, "e4m3")
    out = mxq(h1, 1, "e4m3") @ mxq(w2, 0, "e4m3")
    return np.maximum(f64(scaling) * out + f64(bias), 0.0)

@@ -1,0 +1,327 @@
+from contextlib import ExitStack
+
+import concourse.mybir as mybir
+from concourse.masks import make_identity
+
+F32 = mybir.dt.float32
+BF16 = mybir.dt.bfloat16
+U32 = mybir.dt.uint32
+U8 = mybir.dt.uint8
+FP8X4 = mybir.dt.float8_e4m3fn_x4
+ALU = mybir.AluOpType
+ACT = mybir.ActivationFunctionType
+
+P = 128
+B = 256
+U = 2048
+PACK = 4
+KP = P * PACK
+NG = U // KP
+CW = 512
+NC = U // CW
+NGR = 2 * NG
+FLOPS = 2 * 2 * B * U * U
+
+ROWS2 = [("rows", 0, 2), ("rows", 2, 4)]
+QQH = [("cols", 0, 512), ("cols", 512, 1024), ("cols", 1024, 2048)]
+HH = [("cols", 0, 1024), ("cols", 1024, 2048)]
+HQQ = [("cols", 0, 1024), ("cols", 1024, 1536), ("cols", 1536, 2048)]
+GROUP_CUTS = [QQH, ROWS2, ROWS2, ROWS2, ROWS2, ROWS2, HH, HQQ]
+SB1 = 704
+SB2 = 576
+GROUP_BLOCKS = [
+    [(0, 512, 448), (512, 1024, 448), (1024, 2048, 896)],
+    [(0, 1024, 1024), (1024, 2048, SB1)],
+    [(0, 1024, 1024), (1024, 2048, SB1)],
+    [(0, 1024, 1024), (1024, 2048, SB1)],
+    [(0, 1024, 1024), (1024, 2048, SB2)],
+    [(0, 1024, 1024), (1024, 2048, SB2)],
+    [(0, 1024, 832), (1024, 2048, 832)],
+    [(0, 1024, 768), (1024, 1536, 320), (1536, 2048, 288)],
+]
+LEAD = 1
+K_BUFS = 4
+M_BUFS = 4
+G_BUFS = 4
+H0_AFTER = 6
+H0_STEP = 5
+EVAC_STEPS = [10, 11, 12, 13]
+BIAS_STEP = 1
+
+
+def tile_sparsefactorisationdense_pa_kernel(tc, h0, k1, k2, m1, m2, scaling, bias, out):
+    nc = tc.nc
+    with ExitStack() as ctx:
+        const = ctx.enter_context(tc.tile_pool(name="const", bufs=1))
+        kpool = ctx.enter_context(tc.tile_pool(name="kpool", bufs=K_BUFS))
+        mpool = ctx.enter_context(tc.tile_pool(name="mpool", bufs=M_BUFS))
+        grp = ctx.enter_context(tc.tile_pool(name="grp", bufs=G_BUFS))
+        hgp = ctx.enter_context(tc.tile_pool(name="hgp", bufs=1))
+        cod = ctx.enter_context(tc.tile_pool(name="cod", bufs=6))
+        psum = ctx.enter_context(tc.psum_pool(name="psum", bufs=8))
+        ctx.enter_context(tc.manual_schedule())
+
+        pieces = []
+        blocks = []
+        first_block = {}
+        for i in range(NGR):
+            for cut in GROUP_CUTS[i]:
+                pieces.append((i, cut[0], cut[1], cut[2]))
+            first_block[i] = len(blocks)
+            for blk in GROUP_BLOCKS[i]:
+                blocks.append((i, blk[0], blk[1], blk[2]))
+        first_block[NGR] = len(blocks)
+        NB = len(blocks)
+        ktiles = {}
+        col_src = {}
+        mult_ops = {}
+        codes = {}
+        grouped = {}
+        state = {"loaded": 0, "mults": 0, "regrouped": 0}
+
+        h0_sb = hgp.tile([P, 2 * U], BF16, tag="hx", name="h0_sb")
+
+        def dram_view(x, w, g):
+            return x[g * KP:(g + 1) * KP, :].rearrange("(p j) n -> p j n", j=PACK)
+
+        def load_piece(n):
+            i, kind, a, b = pieces[n]
+            w, g = divmod(i, NG)
+            if i not in ktiles:
+                ktiles[i] = kpool.tile([P, PACK * U], BF16, tag="k", name="kt%d" % i)
+            kt = ktiles[i]
+            mt = mpool.tile([P, 2 * U], BF16, tag="m", name="mt%d" % n)
+            ksrc = dram_view(k1 if w == 0 else k2, w, g)
+            msrc = dram_view(m1 if w == 0 else m2, w, g)
+            if kind == "rows":
+                kh = kt[:, a * U:b * U]
+                mh = mt[:, 0:(b - a) * U]
+                nc.sync.dma_start(out=kh.rearrange("p (j n) -> p j n", j=b - a), in_=ksrc[:, a:b, :])
+                nc.sync.dma_start(out=mh.rearrange("p (j n) -> p j n", j=b - a), in_=msrc[:, a:b, :])
+                col_src[i] = (0, kt[:].rearrange("p (j n) -> p j n", j=PACK))
+            else:
+                kh = kt[:, PACK * a:PACK * b]
+                mh = mt[:, 0:PACK * (b - a)]
+                kv = kh.rearrange("p (j n) -> p j n", j=PACK)
+                nc.sync.dma_start(out=kv, in_=ksrc[:, :, a:b])
+                nc.sync.dma_start(out=mh.rearrange("p (j n) -> p j n", j=PACK), in_=msrc[:, :, a:b])
+                for c in range(a, b, CW):
+                    col_src[(i, c)] = (a, kv)
+            mult_ops[n] = (kh, mh)
+            if n + 1 == H0_AFTER:
+                nc.sync.dma_start(out=h0_sb[:].rearrange("p (a k) -> p a k", a=2),
+                                  in_=h0.rearrange("(a p) k -> p a k", p=P))
+
+        def pump_loads():
+            while state["loaded"] < len(pieces):
+                n = state["loaded"]
+                i = pieces[n][0]
+                if n - M_BUFS >= state["mults"]:
+                    return
+                if i not in ktiles and i >= K_BUFS and first_block[i - K_BUFS + 1] > state["regrouped"]:
+                    return
+                load_piece(n)
+                state["loaded"] = n + 1
+
+        def mult(n):
+            assert n == state["mults"]
+            kh, mh = mult_ops[n]
+            nc.vector.tensor_tensor(out=kh, in0=kh, in1=mh, op=ALU.mult)
+            state["mults"] = n + 1
+            pump_loads()
+
+        brow = const.tile([P, U], BF16, name="brow")
+        nc.vector.memset(brow[:], 0.0)
+        ones = const.tile([P, P], BF16, name="ones")
+        nc.vector.memset(ones[:], 1.0)
+        ident = const.tile([P, P], F32, name="ident")
+        make_identity(nc, ident[:])
+        sc_b = const.tile([P, 1], BF16, name="sc_b")
+        sc_f = const.tile([P, 1], F32, name="sc_f")
+        for n in range(len(GROUP_CUTS[0])):
+            load_piece(n)
+        state["loaded"] = len(GROUP_CUTS[0])
+        nc.sync.dma_start(out=brow[0:1, :], in_=bias.rearrange("(o n) -> o n", o=1))
+        nc.sync.dma_start(out=sc_b[:], in_=scaling.partition_broadcast(P))
+        pump_loads()
+
+        bias_bc = const.tile([P, U], F32, name="bias_bc")
+        pbs = {}
+        for r in range(NC):
+            pbs[r] = psum.tile([P, CW], F32, tag="bank", name="pb%d" % r)
+            nc.tensor.matmul(out=pbs[r][:], lhsT=ones[:], rhs=brow[:, r * CW:(r + 1) * CW], start=True, stop=True)
+
+        def bias_evac(r):
+            nc.scalar.copy(out=bias_bc[:, r * CW:(r + 1) * CW], in_=pbs[r][:])
+
+        h0w = h0_sb[:].bitcast(F32)
+        h0g = hgp.tile([P, NG * B * PACK], BF16, tag="hg", name="h0g", align_bytes=64)
+        h0gw = h0g[:].bitcast(F32)
+        h0c = const.tile([P, NG * B], U32, name="h0c", align_bytes=64)
+        h0s = const.tile([P, NG * B], U8, name="h0s", align_bytes=64)
+        h0x = {}
+
+        def h0_evac(g):
+            h0x[g] = psum.tile([P, 2 * B], F32, tag="bank", name="xt%d" % g)
+            for u in range(2):
+                for a in range(2):
+                    base = a * (U // 2) + g * (KP // 2)
+                    nc.tensor.transpose(h0x[g][:, u * B + a * P:u * B + (a + 1) * P],
+                                        h0w[:, base + u:base + KP // 2:2], ident[:])
+            nc.scalar.copy(out=h0gw[:, g * 2 * B:(g + 1) * 2 * B].rearrange("p (b u) -> p b u", u=2),
+                           in_=h0x[g][:].rearrange("p (u b) -> p b u", u=2))
+
+        def h0_quant():
+            nc.vector.quantize_mx(out=h0c[:].bitcast(FP8X4), scales=h0s[:], in_=h0g[:])
+
+        def src_view(i, a, b):
+            base, kv = col_src[i] if i in col_src else col_src[(i, a - a % CW)]
+            return kv[:, :, a - base:b - base]
+
+        def regroup(s):
+            i, a, b, sc = blocks[s]
+            gt = grp.tile([P, b - a, PACK], BF16, tag="g", name="gt%d" % s, align_bytes=64)
+            grouped[s] = gt
+            if i < NG:
+                for c in range(a, b, CW):
+                    src = src_view(i, c, c + CW).rearrange("p j (m t) -> p t m j", t=PACK)
+                    dst = gt[:, c - a:c - a + CW, :].rearrange("p (t m) j -> p t m j", t=PACK)
+                    ms = max(0, min(CW, a + sc - c)) // PACK
+                    if ms > 0:
+                        nc.scalar.copy(out=dst[:, :, 0:ms, :], in_=src[:, :, 0:ms, :])
+                    if ms < P:
+                        nc.vector.tensor_copy(out=dst[:, :, ms:P, :], in_=src[:, :, ms:P, :])
+                state["regrouped"] = s + 1
+                pump_loads()
+                return
+            nc.scalar.copy(
+                out=gt[:, 0:sc, :].rearrange("p (c i) t -> p c t i", i=4),
+                in_=src_view(i, a, a + sc).rearrange("p t (c i) -> p c t i", i=4))
+            if a + sc < b:
+                nc.vector.tensor_copy(
+                    out=gt[:, sc:b - a, :].rearrange("p (c i) t -> p c t i", i=4),
+                    in_=src_view(i, a + sc, b).rearrange("p t (c i) -> p c t i", i=4))
+            state["regrouped"] = s + 1
+            pump_loads()
+
+        def quantise(s):
+            i, a, b, sc = blocks[s]
+            if a == 0:
+                wc = cod.tile([P, U], U32, tag="wc", name="wc%d" % i, align_bytes=64)
+                ws = cod.tile([P, U], U8, tag="ws", name="ws%d" % i, align_bytes=64)
+                codes[i] = (wc, ws)
+            wc, ws = codes[i]
+            nc.vector.quantize_mx(out=wc[:, a:b].bitcast(FP8X4), scales=ws[:, a:b],
+                                  in_=grouped[s][:].rearrange("p c t -> p (c t)"))
+
+        late = {}
+        h1c = const.tile([P, NG * B], U32, name="h1c", align_bytes=64)
+        h1s = const.tile([P, NG * B], U8, name="h1s", align_bytes=64)
+        h1p = {}
+
+        def mm1(G):
+            for bh in range(2):
+                h1p[(G, bh)] = psum.tile([P, CW], F32, tag="bank", name="h1p%d_%d" % (G, bh))
+            for t in range(PACK):
+                n0 = G * KP + t * P
+                for g in range(NG):
+                    wc, ws = codes[g]
+                    for bh in range(2):
+                        lo = g * B + bh * P
+                        nc.tensor.matmul_mx(
+                            out=h1p[(G, bh)][:, t * P:(t + 1) * P],
+                            lhsT=wc[:, n0:n0 + P].bitcast(FP8X4), lhsT_scale=ws[:, n0:n0 + P],
+                            rhs=h0c[:, lo:lo + P].bitcast(FP8X4), rhs_scale=h0s[:, lo:lo + P],
+                            start=(g == 0), stop=(g == NG - 1))
+
+        def h1_evac(G):
+            if G == 0:
+                late["h1g"] = hgp.tile([P, NG, B, PACK], BF16, tag="hg", name="h1g", align_bytes=64)
+            for bh in range(2):
+                nc.scalar.copy(out=late["h1g"][:, G, bh * P:(bh + 1) * P, :],
+                               in_=h1p[(G, bh)][:].rearrange("p (t b) -> p b t", t=PACK))
+
+        def h1_quant(G0):
+            nc.vector.quantize_mx(out=h1c[:, G0 * B:(G0 + 2) * B].bitcast(FP8X4), scales=h1s[:, G0 * B:(G0 + 2) * B],
+                                  in_=late["h1g"][:, G0:G0 + 2, :, :].rearrange("p g b t -> p (g b t)"))
+
+        acc = {}
+
+        def mm2(i, c):
+            G = i - NG
+            wc, ws = codes[i]
+            lo = c * CW
+            for a in range(2):
+                if G == 0:
+                    acc[(a, c)] = psum.tile([P, CW], F32, tag="bank", name="acc%d_%d" % (a, c))
+                hl = G * B + a * P
+                nc.tensor.matmul_mx(
+                    out=acc[(a, c)][:],
+                    lhsT=h1c[:, hl:hl + P].bitcast(FP8X4), lhsT_scale=h1s[:, hl:hl + P],
+                    rhs=wc[:, lo:lo + CW].bitcast(FP8X4), rhs_scale=ws[:, lo:lo + CW],
+                    start=(G == 0), stop=(G == NG - 1))
+
+        def epilogue(c):
+            lo = c * CW
+            if c == 0:
+                late["o0"] = hgp.tile([P, U], F32, tag="hx", name="o_a0")
+                late["o1"] = hgp.tile([P, U], F32, tag="hg", name="o_a1", align_bytes=64)
+            for a in range(2):
+                o = late["o%d" % a][:, lo:lo + CW]
+                nc.vector.scalar_tensor_tensor(out=o, in0=acc[(a, c)][:], scalar=sc_f[:, 0:1],
+                                               in1=bias_bc[:, lo:lo + CW], op0=ALU.mult, op1=ALU.add)
+                nc.scalar.activation(out=o, in_=o, func=ACT.Relu)
+                nc.sync.dma_start(out=out[a * P:(a + 1) * P, lo:lo + CW], in_=o)
+
+        mult_at = {}
+        for n in range(len(pieces)):
+            i, kind, a, b = pieces[n]
+            if kind == "rows":
+                s = first_block[i] - 2 + a // 2
+            else:
+                s = min(x for x in range(NB) if blocks[x][0] == i and blocks[x][1] >= a) - LEAD
+            s = max(s, 0)
+            mult_at[s] = mult_at.get(s, []) + [n]
+
+        pending = []
+        evacs_done = 0
+        quants_done = 0
+        for s in range(NB + 1):
+            for n in mult_at.get(s, []):
+                mult(n)
+            if s < NB:
+                regroup(s)
+            if s >= 1:
+                quantise(s - 1)
+                i, a, b, sc = blocks[s - 1]
+                if s == first_block[NG]:
+                    for G in range(NG):
+                        mm1(G)
+                if i >= NG:
+                    for c in range(a // CW, b // CW):
+                        pending.append((i, c))
+            if s in (BIAS_STEP, BIAS_STEP + 1):
+                bias_evac(2 * (s - BIAS_STEP))
+                bias_evac(2 * (s - BIAS_STEP) + 1)
+            if s in (H0_STEP, H0_STEP + 1):
+                h0_evac(2 * (s - H0_STEP))
+                h0_evac(2 * (s - H0_STEP) + 1)
+            if s == H0_STEP + 2:
+                h0_quant()
+                nc.vector.tensor_copy(out=sc_f[:], in_=sc_b[:])
+            for G in range(NG):
+                if s == EVAC_STEPS[G]:
+                    h1_evac(G)
+                    evacs_done = 2 * (G + 1)
+                if s == EVAC_STEPS[G] + 1 and G % 2 == 1:
+                    h1_quant(G - 1)
+                    quants_done = G + 1
+            left = []
+            for i, c in pending:
+                if i - NG < quants_done and evacs_done >= 2 * (c + 1) and not left:
+                    mm2(i, c)
+                else:
+                    left.append((i, c))
+            pending = left
+        for c in range(NC):
+            epilogue(c)

@@ -19,34 +19,36 @@ KP = P * PACK
 NG = U // KP
 CW = 512
 NC = U // CW
-NGR = 2 * NG
+HALF = U // 2
 FLOPS = 2 * 2 * B * U * U
 
-ROWS2 = [("rows", 0, 2), ("rows", 2, 4)]
-QQH = [("cols", 0, 512), ("cols", 512, 1024), ("cols", 1024, 2048)]
-HH = [("cols", 0, 1024), ("cols", 1024, 2048)]
-HQQ = [("cols", 0, 1024), ("cols", 1024, 1536), ("cols", 1536, 2048)]
-GROUP_CUTS = [QQH, ROWS2, ROWS2, ROWS2, ROWS2, ROWS2, HH, HQQ]
-SB1 = 704
-SB2 = 576
-GROUP_BLOCKS = [
-    [(0, 512, 448), (512, 1024, 448), (1024, 2048, 896)],
-    [(0, 1024, 1024), (1024, 2048, SB1)],
-    [(0, 1024, 1024), (1024, 2048, SB1)],
-    [(0, 1024, 1024), (1024, 2048, SB1)],
-    [(0, 1024, 1024), (1024, 2048, SB2)],
-    [(0, 1024, 1024), (1024, 2048, SB2)],
-    [(0, 1024, 832), (1024, 2048, 832)],
-    [(0, 1024, 768), (1024, 1536, 320), (1536, 2048, 288)],
+PIECES = [
+    (0, 0, 0, 512, 384),
+    (0, 0, 512, 1024, 384),
+    (0, 0, 1024, 2048, 768),
+    (0, 1, 0, 1024, 768),
+    (0, 1, 1024, 2048, 768),
+    (0, 2, 0, 1024, 768),
+    (0, 2, 1024, 2048, 768),
+    (0, 3, 0, 1024, 768),
+    (0, 3, 1024, 2048, 768),
+    (1, 0, 0, 1024, 576),
+    (1, 1, 0, 1024, 576),
+    (1, 2, 0, 1024, 576),
+    (1, 3, 0, 1024, 704),
+    (1, 0, 1024, 2048, 704),
+    (1, 1, 1024, 2048, 704),
+    (1, 2, 1024, 2048, 704),
+    (1, 3, 1024, 1536, 320),
+    (1, 3, 1536, 2048, 320),
 ]
-LEAD = 1
-K_BUFS = 4
-M_BUFS = 4
-G_BUFS = 4
-H0_AFTER = 6
-H0_STEP = 5
-EVAC_STEPS = [10, 11, 12, 13]
+K_BUFS = 8
+M_BUFS = 6
+H0_AFTER = 3
+H0_STEP = 4
 BIAS_STEP = 1
+FIRST2 = 9
+LAST_A = 12
 
 
 def tile_sparsefactorisationdense_pa_kernel(tc, h0, k1, k2, m1, m2, scaling, bias, out):
@@ -55,80 +57,18 @@ def tile_sparsefactorisationdense_pa_kernel(tc, h0, k1, k2, m1, m2, scaling, bia
         const = ctx.enter_context(tc.tile_pool(name="const", bufs=1))
         kpool = ctx.enter_context(tc.tile_pool(name="kpool", bufs=K_BUFS))
         mpool = ctx.enter_context(tc.tile_pool(name="mpool", bufs=M_BUFS))
-        grp = ctx.enter_context(tc.tile_pool(name="grp", bufs=G_BUFS))
+        grp = ctx.enter_context(tc.tile_pool(name="grp", bufs=3))
         hgp = ctx.enter_context(tc.tile_pool(name="hgp", bufs=1))
         cod = ctx.enter_context(tc.tile_pool(name="cod", bufs=6))
         psum = ctx.enter_context(tc.psum_pool(name="psum", bufs=8))
         ctx.enter_context(tc.manual_schedule())
 
-        pieces = []
-        blocks = []
-        first_block = {}
-        for i in range(NGR):
-            for cut in GROUP_CUTS[i]:
-                pieces.append((i, cut[0], cut[1], cut[2]))
-            first_block[i] = len(blocks)
-            for blk in GROUP_BLOCKS[i]:
-                blocks.append((i, blk[0], blk[1], blk[2]))
-        first_block[NGR] = len(blocks)
-        NB = len(blocks)
-        ktiles = {}
-        col_src = {}
-        mult_ops = {}
-        codes = {}
+        NP = len(PIECES)
+        kt = {}
+        mt = {}
         grouped = {}
+        codes = {}
         state = {"loaded": 0, "mults": 0, "regrouped": 0}
-
-        h0_sb = hgp.tile([P, 2 * U], BF16, tag="hx", name="h0_sb")
-
-        def dram_view(x, w, g):
-            return x[g * KP:(g + 1) * KP, :].rearrange("(p j) n -> p j n", j=PACK)
-
-        def load_piece(n):
-            i, kind, a, b = pieces[n]
-            w, g = divmod(i, NG)
-            if i not in ktiles:
-                ktiles[i] = kpool.tile([P, PACK * U], BF16, tag="k", name="kt%d" % i)
-            kt = ktiles[i]
-            mt = mpool.tile([P, 2 * U], BF16, tag="m", name="mt%d" % n)
-            ksrc = dram_view(k1 if w == 0 else k2, w, g)
-            msrc = dram_view(m1 if w == 0 else m2, w, g)
-            if kind == "rows":
-                kh = kt[:, a * U:b * U]
-                mh = mt[:, 0:(b - a) * U]
-                nc.sync.dma_start(out=kh.rearrange("p (j n) -> p j n", j=b - a), in_=ksrc[:, a:b, :])
-                nc.sync.dma_start(out=mh.rearrange("p (j n) -> p j n", j=b - a), in_=msrc[:, a:b, :])
-                col_src[i] = (0, kt[:].rearrange("p (j n) -> p j n", j=PACK))
-            else:
-                kh = kt[:, PACK * a:PACK * b]
-                mh = mt[:, 0:PACK * (b - a)]
-                kv = kh.rearrange("p (j n) -> p j n", j=PACK)
-                nc.sync.dma_start(out=kv, in_=ksrc[:, :, a:b])
-                nc.sync.dma_start(out=mh.rearrange("p (j n) -> p j n", j=PACK), in_=msrc[:, :, a:b])
-                for c in range(a, b, CW):
-                    col_src[(i, c)] = (a, kv)
-            mult_ops[n] = (kh, mh)
-            if n + 1 == H0_AFTER:
-                nc.sync.dma_start(out=h0_sb[:].rearrange("p (a k) -> p a k", a=2),
-                                  in_=h0.rearrange("(a p) k -> p a k", p=P))
-
-        def pump_loads():
-            while state["loaded"] < len(pieces):
-                n = state["loaded"]
-                i = pieces[n][0]
-                if n - M_BUFS >= state["mults"]:
-                    return
-                if i not in ktiles and i >= K_BUFS and first_block[i - K_BUFS + 1] > state["regrouped"]:
-                    return
-                load_piece(n)
-                state["loaded"] = n + 1
-
-        def mult(n):
-            assert n == state["mults"]
-            kh, mh = mult_ops[n]
-            nc.vector.tensor_tensor(out=kh, in0=kh, in1=mh, op=ALU.mult)
-            state["mults"] = n + 1
-            pump_loads()
 
         brow = const.tile([P, U], BF16, name="brow")
         nc.vector.memset(brow[:], 0.0)
@@ -136,192 +76,204 @@ def tile_sparsefactorisationdense_pa_kernel(tc, h0, k1, k2, m1, m2, scaling, bia
         nc.vector.memset(ones[:], 1.0)
         ident = const.tile([P, P], F32, name="ident")
         make_identity(nc, ident[:])
+        warm = const.tile([P, P], BF16, name="warm")
+        nc.scalar.copy(out=warm[:], in_=ones[:])
         sc_b = const.tile([P, 1], BF16, name="sc_b")
         sc_f = const.tile([P, 1], F32, name="sc_f")
-        for n in range(len(GROUP_CUTS[0])):
-            load_piece(n)
-        state["loaded"] = len(GROUP_CUTS[0])
-        nc.sync.dma_start(out=brow[0:1, :], in_=bias.rearrange("(o n) -> o n", o=1))
-        nc.sync.dma_start(out=sc_b[:], in_=scaling.partition_broadcast(P))
-        pump_loads()
 
-        bias_bc = const.tile([P, U], F32, name="bias_bc")
-        pbs = {}
-        for r in range(NC):
-            pbs[r] = psum.tile([P, CW], F32, tag="bank", name="pb%d" % r)
-            nc.tensor.matmul(out=pbs[r][:], lhsT=ones[:], rhs=brow[:, r * CW:(r + 1) * CW], start=True, stop=True)
+        h0_sb = hgp.tile([P, 2 * U], BF16, tag="hx", name="h0_sb")
 
-        def bias_evac(r):
-            nc.scalar.copy(out=bias_bc[:, r * CW:(r + 1) * CW], in_=pbs[r][:])
+        def load_piece(n):
+            w, g, a, b, sc = PIECES[n]
+            x, m = (k1, m1) if w == 0 else (k2, m2)
+            rows = slice(g * KP, (g + 1) * KP)
+            kt[n] = kpool.tile([P, PACK * HALF], BF16, tag="k", name="kt%d" % n)
+            mt[n] = mpool.tile([P, PACK * HALF], BF16, tag="m", name="mt%d" % n)
+            for dst, src in ((kt[n], x), (mt[n], m)):
+                nc.sync.dma_start(out=dst[:, 0:PACK * (b - a)].rearrange("p (j n) -> p j n", j=PACK),
+                                  in_=src[rows, a:b].rearrange("(p j) n -> p j n", j=PACK))
+            if n == 0:
+                nc.sync.dma_start(out=brow[0:1, :], in_=bias.rearrange("(o n) -> o n", o=1))
+                nc.sync.dma_start(out=sc_b[:], in_=scaling.partition_broadcast(P))
+            if n + 1 == H0_AFTER:
+                nc.sync.dma_start(out=h0_sb[:].rearrange("p (a k) -> p a k", a=2),
+                                  in_=h0.rearrange("(a p) k -> p a k", p=P))
+            state["loaded"] = n + 1
 
-        h0w = h0_sb[:].bitcast(F32)
-        h0g = hgp.tile([P, NG * B * PACK], BF16, tag="hg", name="h0g", align_bytes=64)
-        h0gw = h0g[:].bitcast(F32)
-        h0c = const.tile([P, NG * B], U32, name="h0c", align_bytes=64)
-        h0s = const.tile([P, NG * B], U8, name="h0s", align_bytes=64)
-        h0x = {}
+        def pump_loads():
+            while (state["loaded"] < NP and state["loaded"] < state["mults"] + M_BUFS
+                   and state["loaded"] < state["regrouped"] + K_BUFS):
+                load_piece(state["loaded"])
 
-        def h0_evac(g):
-            h0x[g] = psum.tile([P, 2 * B], F32, tag="bank", name="xt%d" % g)
+        def mult(n):
+            w, g, a, b, sc = PIECES[n]
+            e = PACK * (b - a)
+            nc.vector.tensor_tensor(out=kt[n][:, 0:e], in0=kt[n][:, 0:e], in1=mt[n][:, 0:e], op=ALU.mult)
+            state["mults"] = n + 1
+            pump_loads()
+
+        def regroup_part(n, engine_copy, lo, hi):
+            w, g, a, b, sc = PIECES[n]
+            src = kt[n][:, 0:PACK * (b - a)].rearrange("p (j n) -> p j n", j=PACK)
+            engine_copy(out=grouped[n][:, lo:hi, :].rearrange("p (c i) j -> p c j i", i=4),
+                        in_=src[:, :, lo:hi].rearrange("p j (c i) -> p c j i", i=4))
+
+        def regroup_scalar(n):
+            w, g, a, b, sc = PIECES[n]
+            grouped[n] = grp.tile([P, HALF, PACK], BF16, tag="g", name="gt%d" % n, align_bytes=64)
+            regroup_part(n, nc.scalar.copy, 0, sc)
+
+        def regroup_vector(n):
+            w, g, a, b, sc = PIECES[n]
+            if sc < b - a:
+                regroup_part(n, nc.vector.tensor_copy, sc, b - a)
+            state["regrouped"] = n + 1
+            pump_loads()
+
+        def quantise(n):
+            w, g, a, b, sc = PIECES[n]
+            wc = cod.tile([P, HALF], U32, tag="wc", name="wc%d" % n, align_bytes=64)
+            ws = cod.tile([P, HALF], U8, tag="ws", name="ws%d" % n, align_bytes=64)
+            codes[n] = (wc, ws)
+            nc.vector.quantize_mx(out=wc[:, 0:b - a].bitcast(FP8X4), scales=ws[:, 0:b - a],
+                                  in_=grouped[n][:, 0:b - a, :].rearrange("p c j -> p (c j)"))
+
+        def transpose_pass(words, g, name):
+            xt = psum.tile([P, 2 * B], F32, tag="bank", name=name)
             for u in range(2):
                 for a in range(2):
                     base = a * (U // 2) + g * (KP // 2)
-                    nc.tensor.transpose(h0x[g][:, u * B + a * P:u * B + (a + 1) * P],
-                                        h0w[:, base + u:base + KP // 2:2], ident[:])
-            nc.scalar.copy(out=h0gw[:, g * 2 * B:(g + 1) * 2 * B].rearrange("p (b u) -> p b u", u=2),
-                           in_=h0x[g][:].rearrange("p (u b) -> p b u", u=2))
+                    nc.tensor.transpose(xt[:, u * B + a * P:u * B + (a + 1) * P],
+                                        words[:, base + u:base + KP // 2:2], ident[:])
+            return xt
 
-        def h0_quant():
-            nc.vector.quantize_mx(out=h0c[:].bitcast(FP8X4), scales=h0s[:], in_=h0g[:])
+        def evac_pass(xt, dst_words, g):
+            nc.scalar.copy(out=dst_words[:, g * 2 * B:(g + 1) * 2 * B].rearrange("p (b u) -> p b u", u=2),
+                           in_=xt[:].rearrange("p (u b) -> p b u", u=2))
 
-        def src_view(i, a, b):
-            base, kv = col_src[i] if i in col_src else col_src[(i, a - a % CW)]
-            return kv[:, :, a - base:b - base]
-
-        def regroup(s):
-            i, a, b, sc = blocks[s]
-            gt = grp.tile([P, b - a, PACK], BF16, tag="g", name="gt%d" % s, align_bytes=64)
-            grouped[s] = gt
-            if i < NG:
-                for c in range(a, b, CW):
-                    src = src_view(i, c, c + CW).rearrange("p j (m t) -> p t m j", t=PACK)
-                    dst = gt[:, c - a:c - a + CW, :].rearrange("p (t m) j -> p t m j", t=PACK)
-                    ms = max(0, min(CW, a + sc - c)) // PACK
-                    if ms > 0:
-                        nc.scalar.copy(out=dst[:, :, 0:ms, :], in_=src[:, :, 0:ms, :])
-                    if ms < P:
-                        nc.vector.tensor_copy(out=dst[:, :, ms:P, :], in_=src[:, :, ms:P, :])
-                state["regrouped"] = s + 1
-                pump_loads()
-                return
-            nc.scalar.copy(
-                out=gt[:, 0:sc, :].rearrange("p (c i) t -> p c t i", i=4),
-                in_=src_view(i, a, a + sc).rearrange("p t (c i) -> p c t i", i=4))
-            if a + sc < b:
-                nc.vector.tensor_copy(
-                    out=gt[:, sc:b - a, :].rearrange("p (c i) t -> p c t i", i=4),
-                    in_=src_view(i, a + sc, b).rearrange("p t (c i) -> p c t i", i=4))
-            state["regrouped"] = s + 1
-            pump_loads()
-
-        def quantise(s):
-            i, a, b, sc = blocks[s]
-            if a == 0:
-                wc = cod.tile([P, U], U32, tag="wc", name="wc%d" % i, align_bytes=64)
-                ws = cod.tile([P, U], U8, tag="ws", name="ws%d" % i, align_bytes=64)
-                codes[i] = (wc, ws)
-            wc, ws = codes[i]
-            nc.vector.quantize_mx(out=wc[:, a:b].bitcast(FP8X4), scales=ws[:, a:b],
-                                  in_=grouped[s][:].rearrange("p c t -> p (c t)"))
-
-        late = {}
+        h0c = const.tile([P, NG * B], U32, name="h0c", align_bytes=64)
+        h0s = const.tile([P, NG * B], U8, name="h0s", align_bytes=64)
         h1c = const.tile([P, NG * B], U32, name="h1c", align_bytes=64)
         h1s = const.tile([P, NG * B], U8, name="h1s", align_bytes=64)
-        h1p = {}
+        h0g = hgp.tile([P, NG * B * PACK], BF16, tag="hg", name="h0g", align_bytes=64)
 
-        def mm1(G):
-            for bh in range(2):
-                h1p[(G, bh)] = psum.tile([P, CW], F32, tag="bank", name="h1p%d_%d" % (G, bh))
-            for t in range(PACK):
-                n0 = G * KP + t * P
-                for g in range(NG):
-                    wc, ws = codes[g]
-                    for bh in range(2):
-                        lo = g * B + bh * P
-                        nc.tensor.matmul_mx(
-                            out=h1p[(G, bh)][:, t * P:(t + 1) * P],
-                            lhsT=wc[:, n0:n0 + P].bitcast(FP8X4), lhsT_scale=ws[:, n0:n0 + P],
-                            rhs=h0c[:, lo:lo + P].bitcast(FP8X4), rhs_scale=h0s[:, lo:lo + P],
-                            start=(g == 0), stop=(g == NG - 1))
+        acc1 = {}
+        acc2 = {}
 
-        def h1_evac(G):
-            if G == 0:
-                late["h1g"] = hgp.tile([P, NG, B, PACK], BF16, tag="hg", name="h1g", align_bytes=64)
-            for bh in range(2):
-                nc.scalar.copy(out=late["h1g"][:, G, bh * P:(bh + 1) * P, :],
-                               in_=h1p[(G, bh)][:].rearrange("p (t b) -> p b t", t=PACK))
+        def matmuls(n):
+            w, g, a0, b0, sc = PIECES[n]
+            lc, ls, acc = (h0c, h0s, acc1) if w == 0 else (h1c, h1s, acc2)
+            wc, ws = codes[n]
+            for c in range(a0 // CW, b0 // CW):
+                lo = c * CW - a0
+                for a in range(2):
+                    if g == 0:
+                        acc[(a, c)] = psum.tile([P, CW], F32, tag="bank", name="acc%d_%d_%d" % (w, a, c))
+                    hl = g * B + a * P
+                    nc.tensor.matmul_mx(
+                        out=acc[(a, c)][:],
+                        lhsT=lc[:, hl:hl + P].bitcast(FP8X4), lhsT_scale=ls[:, hl:hl + P],
+                        rhs=wc[:, lo:lo + CW].bitcast(FP8X4), rhs_scale=ws[:, lo:lo + CW],
+                        start=(g == 0), stop=(g == NG - 1))
 
-        def h1_quant(G0):
-            nc.vector.quantize_mx(out=h1c[:, G0 * B:(G0 + 2) * B].bitcast(FP8X4), scales=h1s[:, G0 * B:(G0 + 2) * B],
-                                  in_=late["h1g"][:, G0:G0 + 2, :, :].rearrange("p g b t -> p (g b t)"))
+        late = {}
 
-        acc = {}
-
-        def mm2(i, c):
-            G = i - NG
-            wc, ws = codes[i]
-            lo = c * CW
-            for a in range(2):
-                if G == 0:
-                    acc[(a, c)] = psum.tile([P, CW], F32, tag="bank", name="acc%d_%d" % (a, c))
-                hl = G * B + a * P
-                nc.tensor.matmul_mx(
-                    out=acc[(a, c)][:],
-                    lhsT=h1c[:, hl:hl + P].bitcast(FP8X4), lhsT_scale=h1s[:, hl:hl + P],
-                    rhs=wc[:, lo:lo + CW].bitcast(FP8X4), rhs_scale=ws[:, lo:lo + CW],
-                    start=(G == 0), stop=(G == NG - 1))
-
-        def epilogue(c):
-            lo = c * CW
+        def h1_evac(c):
             if c == 0:
-                late["o0"] = hgp.tile([P, U], F32, tag="hx", name="o_a0")
-                late["o1"] = hgp.tile([P, U], F32, tag="hg", name="o_a1", align_bytes=64)
+                late["h1"] = hgp.tile([P, 2 * U], BF16, tag="hx", name="h1_sb")
             for a in range(2):
-                o = late["o%d" % a][:, lo:lo + CW]
-                nc.vector.scalar_tensor_tensor(out=o, in0=acc[(a, c)][:], scalar=sc_f[:, 0:1],
-                                               in1=bias_bc[:, lo:lo + CW], op0=ALU.mult, op1=ALU.add)
+                nc.scalar.copy(out=late["h1"][:, a * U + c * CW:a * U + (c + 1) * CW], in_=acc1[(a, c)][:])
+
+        def h1_transpose(g):
+            late["xt%d" % g] = transpose_pass(late["h1"][:].bitcast(F32), g, "yt%d" % g)
+
+        def h1_regroup(g):
+            if g == 0:
+                late["h1g"] = hgp.tile([P, NG * B * PACK], BF16, tag="hg", name="h1g", align_bytes=64)
+            evac_pass(late["xt%d" % g], late["h1g"][:].bitcast(F32), g)
+
+        def h1_quant(g0):
+            lo, hi = g0 * B, (g0 + 2) * B
+            nc.vector.quantize_mx(out=h1c[:, lo:hi].bitcast(FP8X4), scales=h1s[:, lo:hi],
+                                  in_=late["h1g"][:, lo * PACK:hi * PACK])
+
+        osb = const.tile([P, 2 * U], F32, name="osb")
+
+        def finish_gain(c):
+            for a in range(2):
+                nc.vector.scalar_tensor_tensor(out=osb[:, a * U + c * CW:a * U + (c + 1) * CW], in0=acc2[(a, c)][:],
+                                               scalar=sc_f[:, 0:1], in1=bias_bc[:, c * CW:(c + 1) * CW],
+                                               op0=ALU.mult, op1=ALU.add)
+
+        def finish_relu(c):
+            for a in range(2):
+                o = osb[:, a * U + c * CW:a * U + (c + 1) * CW]
                 nc.scalar.activation(out=o, in_=o, func=ACT.Relu)
-                nc.sync.dma_start(out=out[a * P:(a + 1) * P, lo:lo + CW], in_=o)
+                nc.sync.dma_start(out=out[a * P:(a + 1) * P, c * CW:(c + 1) * CW], in_=o)
 
-        mult_at = {}
-        for n in range(len(pieces)):
-            i, kind, a, b = pieces[n]
-            if kind == "rows":
-                s = first_block[i] - 2 + a // 2
-            else:
-                s = min(x for x in range(NB) if blocks[x][0] == i and blocks[x][1] >= a) - LEAD
-            s = max(s, 0)
-            mult_at[s] = mult_at.get(s, []) + [n]
+        bias_bc = const.tile([P, U], F32, name="bias_bc")
 
+        pump_loads()
         pending = []
-        evacs_done = 0
-        quants_done = 0
-        for s in range(NB + 1):
-            for n in mult_at.get(s, []):
-                mult(n)
-            if s < NB:
-                regroup(s)
+        for s in range(NP + 1):
+            if s == 0:
+                mult(0)
+            if s < NP:
+                regroup_scalar(s)
             if s >= 1:
                 quantise(s - 1)
-                i, a, b, sc = blocks[s - 1]
-                if s == first_block[NG]:
-                    for G in range(NG):
-                        mm1(G)
-                if i >= NG:
-                    for c in range(a // CW, b // CW):
-                        pending.append((i, c))
-            if s in (BIAS_STEP, BIAS_STEP + 1):
-                bias_evac(2 * (s - BIAS_STEP))
-                bias_evac(2 * (s - BIAS_STEP) + 1)
-            if s in (H0_STEP, H0_STEP + 1):
-                h0_evac(2 * (s - H0_STEP))
-                h0_evac(2 * (s - H0_STEP) + 1)
-            if s == H0_STEP + 2:
-                h0_quant()
+            if s < NP:
+                regroup_vector(s)
+            if s + 1 < NP:
+                mult(s + 1)
+            if s >= 1:
+                pending.append(s - 1)
+            if s == BIAS_STEP:
+                pbs = []
+                for r in range(NC):
+                    pb = psum.tile([P, CW], F32, tag="bank", name="pb%d" % r)
+                    nc.tensor.matmul(out=pb[:], lhsT=ones[:], rhs=brow[:, r * CW:(r + 1) * CW], start=True, stop=True)
+                    pbs.append(pb)
+                for r in range(NC):
+                    nc.scalar.copy(out=bias_bc[:, r * CW:(r + 1) * CW], in_=pbs[r][:])
                 nc.vector.tensor_copy(out=sc_f[:], in_=sc_b[:])
-            for G in range(NG):
-                if s == EVAC_STEPS[G]:
-                    h1_evac(G)
-                    evacs_done = 2 * (G + 1)
-                if s == EVAC_STEPS[G] + 1 and G % 2 == 1:
-                    h1_quant(G - 1)
-                    quants_done = G + 1
+            if s == H0_STEP:
+                xts = [transpose_pass(h0_sb[:].bitcast(F32), g, "xt%d" % g) for g in range(NG)]
+                for g in range(NG):
+                    evac_pass(xts[g], h0g[:].bitcast(F32), g)
+            if s == H0_STEP + 1:
+                nc.vector.quantize_mx(out=h0c[:].bitcast(FP8X4), scales=h0s[:], in_=h0g[:])
+            if s == FIRST2 + 3:
+                h1_quant(2)
             left = []
-            for i, c in pending:
-                if i - NG < quants_done and evacs_done >= 2 * (c + 1) and not left:
-                    mm2(i, c)
+            for n in pending:
+                if PIECES[n][0] == 0 and s > H0_STEP or PIECES[n][0] == 1 and s >= FIRST2 + 3:
+                    matmuls(n)
                 else:
-                    left.append((i, c))
+                    left.append(n)
             pending = left
-        for c in range(NC):
-            epilogue(c)
+            if s == FIRST2:
+                h1_evac(0)
+                h1_evac(1)
+                h1_transpose(0)
+                h1_transpose(1)
+            if s == FIRST2 + 1:
+                h1_evac(2)
+                h1_evac(3)
+                h1_transpose(2)
+                h1_transpose(3)
+                h1_regroup(0)
+                h1_regroup(1)
+            if s == FIRST2 + 2:
+                h1_regroup(2)
+                h1_regroup(3)
+                h1_quant(0)
+            if s == LAST_A + 2:
+                for c in range(2):
+                    finish_gain(c)
+                    finish_relu(c)
+            if s == NP - 1:
+                finish_gain(2)
+                finish_relu(2)
+        finish_gain(3)
+        finish_relu(3)

@@ -22,7 +22,7 @@ NC = U // CW
 HALF = U // 2
 FLOPS = 2 * 2 * B * U * U
 
-PIECES = [
+BLOCKS = [
     (0, 0, 0, 512, 384),
     (0, 0, 512, 1024, 384),
     (0, 0, 1024, 2048, 768),
@@ -42,13 +42,33 @@ PIECES = [
     (1, 3, 1024, 1536, 320),
     (1, 3, 1536, 2048, 320),
 ]
-K_BUFS = 8
+LOADS = [
+    (0, 0, 0, 4, 0, 512),
+    (0, 0, 0, 4, 512, 1024),
+    (0, 0, 0, 4, 1024, 2048),
+    (0, 1, 0, 2, 0, 2048),
+    (0, 1, 2, 4, 0, 2048),
+    (0, 2, 0, 2, 0, 2048),
+    (0, 2, 2, 4, 0, 2048),
+    (0, 3, 0, 2, 0, 2048),
+    (0, 3, 2, 4, 0, 2048),
+    (1, 0, 0, 4, 0, 1024),
+    (1, 1, 0, 4, 0, 1024),
+    (1, 2, 0, 4, 0, 1024),
+    (1, 3, 0, 4, 0, 1024),
+    (1, 0, 0, 4, 1024, 2048),
+    (1, 1, 0, 4, 1024, 2048),
+    (1, 2, 0, 4, 1024, 2048),
+    (1, 3, 0, 4, 1024, 1536),
+    (1, 3, 0, 4, 1536, 2048),
+]
+K_BUFS = 4
 M_BUFS = 6
 H0_AFTER = 3
 H0_STEP = 4
 BIAS_STEP = 1
-FIRST2 = 9
-LAST_A = 12
+FIRST2 = [x[0] for x in BLOCKS].index(1)
+LAST_A = max(n for n, x in enumerate(BLOCKS) if x[2] < HALF)
 
 
 def tile_sparsefactorisationdense_pa_kernel(tc, h0, k1, k2, m1, m2, scaling, bias, out):
@@ -63,9 +83,11 @@ def tile_sparsefactorisationdense_pa_kernel(tc, h0, k1, k2, m1, m2, scaling, bia
         psum = ctx.enter_context(tc.psum_pool(name="psum", bufs=8))
         ctx.enter_context(tc.manual_schedule())
 
-        NP = len(PIECES)
-        kt = {}
-        mt = {}
+        NB = len(BLOCKS)
+        ktiles = {}
+        src_views = {}
+        mult_ops = {}
+        mult_at = {}
         grouped = {}
         codes = {}
         state = {"loaded": 0, "mults": 0, "regrouped": 0}
@@ -83,15 +105,29 @@ def tile_sparsefactorisationdense_pa_kernel(tc, h0, k1, k2, m1, m2, scaling, bia
 
         h0_sb = hgp.tile([P, 2 * U], BF16, tag="hx", name="h0_sb")
 
-        def load_piece(n):
-            w, g, a, b, sc = PIECES[n]
+        def load(n):
+            w, g, ja, jb, a, b = LOADS[n]
             x, m = (k1, m1) if w == 0 else (k2, m2)
             rows = slice(g * KP, (g + 1) * KP)
-            kt[n] = kpool.tile([P, PACK * HALF], BF16, tag="k", name="kt%d" % n)
-            mt[n] = mpool.tile([P, PACK * HALF], BF16, tag="m", name="mt%d" % n)
-            for dst, src in ((kt[n], x), (mt[n], m)):
-                nc.sync.dma_start(out=dst[:, 0:PACK * (b - a)].rearrange("p (j n) -> p j n", j=PACK),
-                                  in_=src[rows, a:b].rearrange("(p j) n -> p j n", j=PACK))
+            key = (w, g) if w == 0 else (w, a < HALF, g // 2)
+            if key not in ktiles:
+                ktiles[key] = kpool.tile([P, PACK * U], BF16, tag="k", name="kt%d" % n)
+            kt = ktiles[key]
+            mt = mpool.tile([P, PACK * HALF], BF16, tag="m", name="mt%d" % n)
+            e = (jb - ja) * (b - a)
+            if jb - ja < PACK:
+                lo = ja * U
+                src_views[(w, g)] = (kt[:].rearrange("p (j n) -> p j n", j=PACK), 0)
+            else:
+                lo = PACK * a if w == 0 else PACK * (HALF * (g % 2) + a % HALF)
+                view = kt[:, lo:lo + e].rearrange("p (j n) -> p j n", j=PACK)
+                src_views[(w, g, a)] = (view, a)
+            kh = kt[:, lo:lo + e]
+            mh = mt[:, 0:e]
+            for dst, src in ((kh, x), (mh, m)):
+                nc.sync.dma_start(out=dst.rearrange("p (j n) -> p j n", j=jb - ja),
+                                  in_=src[rows, a:b].rearrange("(p j) n -> p j n", j=PACK)[:, ja:jb, :])
+            mult_ops[n] = (kh, mh)
             if n == 0:
                 nc.sync.dma_start(out=brow[0:1, :], in_=bias.rearrange("(o n) -> o n", o=1))
                 nc.sync.dma_start(out=sc_b[:], in_=scaling.partition_broadcast(P))
@@ -100,38 +136,60 @@ def tile_sparsefactorisationdense_pa_kernel(tc, h0, k1, k2, m1, m2, scaling, bia
                                   in_=h0.rearrange("(a p) k -> p a k", p=P))
             state["loaded"] = n + 1
 
+        def last_block(w, g, a, b):
+            return max(n for n, x in enumerate(BLOCKS) if x[0] == w and x[1] == g and a <= x[2] < b)
+
+        tile_order = []
+        tile_last = {}
+        for n in range(len(LOADS)):
+            w, g, ja, jb, a, b = LOADS[n]
+            key = (w, g) if w == 0 else (w, a < HALF, g // 2)
+            if key not in tile_order:
+                tile_order.append(key)
+            tile_last[key] = last_block(w, g, a, b)
+            first = min(i for i, x in enumerate(BLOCKS) if x[0] == w and x[1] == g and a <= x[2] < b)
+            step = max(first - 1 - (1 if jb < PACK else 0), -1)
+            mult_at.setdefault(step, []).append(n)
+
         def pump_loads():
-            while (state["loaded"] < NP and state["loaded"] < state["mults"] + M_BUFS
-                   and state["loaded"] < state["regrouped"] + K_BUFS):
-                load_piece(state["loaded"])
+            while state["loaded"] < len(LOADS):
+                n = state["loaded"]
+                w, g, ja, jb, a, b = LOADS[n]
+                key = (w, g) if w == 0 else (w, a < HALF, g // 2)
+                if n >= state["mults"] + M_BUFS:
+                    return
+                t = tile_order.index(key)
+                if key not in ktiles and t >= K_BUFS and tile_last[tile_order[t - K_BUFS]] >= state["regrouped"]:
+                    return
+                load(n)
 
         def mult(n):
-            w, g, a, b, sc = PIECES[n]
-            e = PACK * (b - a)
-            nc.vector.tensor_tensor(out=kt[n][:, 0:e], in0=kt[n][:, 0:e], in1=mt[n][:, 0:e], op=ALU.mult)
+            kh, mh = mult_ops[n]
+            nc.vector.tensor_tensor(out=kh, in0=kh, in1=mh, op=ALU.mult)
             state["mults"] = n + 1
             pump_loads()
 
         def regroup_part(n, engine_copy, lo, hi):
-            w, g, a, b, sc = PIECES[n]
-            src = kt[n][:, 0:PACK * (b - a)].rearrange("p (j n) -> p j n", j=PACK)
+            w, g, a, b, sc = BLOCKS[n]
+            view, first = src_views[(w, g, a)] if (w, g, a) in src_views else src_views[(w, g)]
+            src = view[:, :, a - first:b - first]
             engine_copy(out=grouped[n][:, lo:hi, :].rearrange("p (c i) j -> p c j i", i=4),
                         in_=src[:, :, lo:hi].rearrange("p j (c i) -> p c j i", i=4))
 
         def regroup_scalar(n):
-            w, g, a, b, sc = PIECES[n]
+            w, g, a, b, sc = BLOCKS[n]
             grouped[n] = grp.tile([P, HALF, PACK], BF16, tag="g", name="gt%d" % n, align_bytes=64)
             regroup_part(n, nc.scalar.copy, 0, sc)
 
         def regroup_vector(n):
-            w, g, a, b, sc = PIECES[n]
+            w, g, a, b, sc = BLOCKS[n]
             if sc < b - a:
                 regroup_part(n, nc.vector.tensor_copy, sc, b - a)
             state["regrouped"] = n + 1
             pump_loads()
 
         def quantise(n):
-            w, g, a, b, sc = PIECES[n]
+            w, g, a, b, sc = BLOCKS[n]
             wc = cod.tile([P, HALF], U32, tag="wc", name="wc%d" % n, align_bytes=64)
             ws = cod.tile([P, HALF], U8, tag="ws", name="ws%d" % n, align_bytes=64)
             codes[n] = (wc, ws)
@@ -161,7 +219,7 @@ def tile_sparsefactorisationdense_pa_kernel(tc, h0, k1, k2, m1, m2, scaling, bia
         acc2 = {}
 
         def matmuls(n):
-            w, g, a0, b0, sc = PIECES[n]
+            w, g, a0, b0, sc = BLOCKS[n]
             lc, ls, acc = (h0c, h0s, acc1) if w == 0 else (h1c, h1s, acc2)
             wc, ws = codes[n]
             for c in range(a0 // CW, b0 // CW):
@@ -197,17 +255,18 @@ def tile_sparsefactorisationdense_pa_kernel(tc, h0, k1, k2, m1, m2, scaling, bia
             nc.vector.quantize_mx(out=h1c[:, lo:hi].bitcast(FP8X4), scales=h1s[:, lo:hi],
                                   in_=late["h1g"][:, lo * PACK:hi * PACK])
 
-        osb = const.tile([P, 2 * U], F32, name="osb")
-
         def finish_gain(c):
+            if c == 0:
+                late["o0"] = hgp.tile([P, U], F32, tag="hx", name="o0")
+                late["o1"] = hgp.tile([P, U], F32, tag="hg", name="o1", align_bytes=64)
             for a in range(2):
-                nc.vector.scalar_tensor_tensor(out=osb[:, a * U + c * CW:a * U + (c + 1) * CW], in0=acc2[(a, c)][:],
+                nc.vector.scalar_tensor_tensor(out=late["o%d" % a][:, c * CW:(c + 1) * CW], in0=acc2[(a, c)][:],
                                                scalar=sc_f[:, 0:1], in1=bias_bc[:, c * CW:(c + 1) * CW],
                                                op0=ALU.mult, op1=ALU.add)
 
         def finish_relu(c):
             for a in range(2):
-                o = osb[:, a * U + c * CW:a * U + (c + 1) * CW]
+                o = late["o%d" % a][:, c * CW:(c + 1) * CW]
                 nc.scalar.activation(out=o, in_=o, func=ACT.Relu)
                 nc.sync.dma_start(out=out[a * P:(a + 1) * P, c * CW:(c + 1) * CW], in_=o)
 
@@ -215,17 +274,18 @@ def tile_sparsefactorisationdense_pa_kernel(tc, h0, k1, k2, m1, m2, scaling, bia
 
         pump_loads()
         pending = []
-        for s in range(NP + 1):
+        for s in range(NB + 1):
             if s == 0:
-                mult(0)
-            if s < NP:
+                for n in mult_at[-1]:
+                    mult(n)
+            if s < NB:
                 regroup_scalar(s)
             if s >= 1:
                 quantise(s - 1)
-            if s < NP:
+            if s < NB:
                 regroup_vector(s)
-            if s + 1 < NP:
-                mult(s + 1)
+            for n in mult_at.get(s, []):
+                mult(n)
             if s >= 1:
                 pending.append(s - 1)
             if s == BIAS_STEP:
@@ -247,7 +307,7 @@ def tile_sparsefactorisationdense_pa_kernel(tc, h0, k1, k2, m1, m2, scaling, bia
                 h1_quant(2)
             left = []
             for n in pending:
-                if PIECES[n][0] == 0 and s > H0_STEP or PIECES[n][0] == 1 and s >= FIRST2 + 3:
+                if BLOCKS[n][0] == 0 and s > H0_STEP or BLOCKS[n][0] == 1 and s >= FIRST2 + 3:
                     matmuls(n)
                 else:
                     left.append(n)
@@ -272,7 +332,7 @@ def tile_sparsefactorisationdense_pa_kernel(tc, h0, k1, k2, m1, m2, scaling, bia
                 for c in range(2):
                     finish_gain(c)
                     finish_relu(c)
-            if s == NP - 1:
+            if s == NB - 1:
                 finish_gain(2)
                 finish_relu(2)
         finish_gain(3)

@@ -25,22 +25,22 @@ FLOPS = 2 * 2 * B * U * U
 BLOCKS = [
     (0, 0, 0, 512, 384),
     (0, 0, 512, 1024, 384),
-    (0, 0, 1024, 2048, 768),
-    (0, 1, 0, 1024, 768),
-    (0, 1, 1024, 2048, 768),
-    (0, 2, 0, 1024, 768),
-    (0, 2, 1024, 2048, 768),
-    (0, 3, 0, 1024, 768),
-    (0, 3, 1024, 2048, 768),
-    (1, 0, 0, 1024, 576),
-    (1, 1, 0, 1024, 576),
-    (1, 2, 0, 1024, 576),
-    (1, 3, 0, 1024, 704),
-    (1, 0, 1024, 2048, 704),
-    (1, 1, 1024, 2048, 704),
-    (1, 2, 1024, 2048, 704),
-    (1, 3, 1024, 1536, 320),
-    (1, 3, 1536, 2048, 320),
+    (0, 0, 1024, 2048, 832),
+    (0, 1, 0, 1024, 832),
+    (0, 1, 1024, 2048, 832),
+    (0, 2, 0, 1024, 832),
+    (0, 2, 1024, 2048, 832),
+    (0, 3, 0, 1024, 832),
+    (0, 3, 1024, 2048, 832),
+    (1, 0, 0, 1024, 640),
+    (1, 0, 1024, 2048, 640),
+    (1, 1, 0, 1024, 640),
+    (1, 1, 1024, 2048, 640),
+    (1, 2, 0, 1024, 768),
+    (1, 2, 1024, 2048, 768),
+    (1, 3, 0, 1024, 768),
+    (1, 3, 1024, 1536, 384),
+    (1, 3, 1536, 2048, 384),
 ]
 LOADS = [
     (0, 0, 0, 4, 0, 512),
@@ -52,13 +52,13 @@ LOADS = [
     (0, 2, 2, 4, 0, 2048),
     (0, 3, 0, 2, 0, 2048),
     (0, 3, 2, 4, 0, 2048),
-    (1, 0, 0, 4, 0, 1024),
-    (1, 1, 0, 4, 0, 1024),
-    (1, 2, 0, 4, 0, 1024),
+    (1, 0, 0, 2, 0, 2048),
+    (1, 0, 2, 4, 0, 2048),
+    (1, 1, 0, 2, 0, 2048),
+    (1, 1, 2, 4, 0, 2048),
+    (1, 2, 0, 2, 0, 2048),
+    (1, 2, 2, 4, 0, 2048),
     (1, 3, 0, 4, 0, 1024),
-    (1, 0, 0, 4, 1024, 2048),
-    (1, 1, 0, 4, 1024, 2048),
-    (1, 2, 0, 4, 1024, 2048),
     (1, 3, 0, 4, 1024, 1536),
     (1, 3, 0, 4, 1536, 2048),
 ]
@@ -68,7 +68,6 @@ H0_AFTER = 3
 H0_STEP = 4
 BIAS_STEP = 1
 FIRST2 = [x[0] for x in BLOCKS].index(1)
-LAST_A = max(n for n, x in enumerate(BLOCKS) if x[2] < HALF)
 
 
 def tile_sparsefactorisationdense_pa_kernel(tc, h0, k1, k2, m1, m2, scaling, bias, out):
@@ -109,7 +108,7 @@ def tile_sparsefactorisationdense_pa_kernel(tc, h0, k1, k2, m1, m2, scaling, bia
             w, g, ja, jb, a, b = LOADS[n]
             x, m = (k1, m1) if w == 0 else (k2, m2)
             rows = slice(g * KP, (g + 1) * KP)
-            key = (w, g) if w == 0 else (w, a < HALF, g // 2)
+            key = (w, g)
             if key not in ktiles:
                 ktiles[key] = kpool.tile([P, PACK * U], BF16, tag="k", name="kt%d" % n)
             kt = ktiles[key]
@@ -119,7 +118,7 @@ def tile_sparsefactorisationdense_pa_kernel(tc, h0, k1, k2, m1, m2, scaling, bia
                 lo = ja * U
                 src_views[(w, g)] = (kt[:].rearrange("p (j n) -> p j n", j=PACK), 0)
             else:
-                lo = PACK * a if w == 0 else PACK * (HALF * (g % 2) + a % HALF)
+                lo = PACK * a
                 view = kt[:, lo:lo + e].rearrange("p (j n) -> p j n", j=PACK)
                 src_views[(w, g, a)] = (view, a)
             kh = kt[:, lo:lo + e]
@@ -143,10 +142,10 @@ def tile_sparsefactorisationdense_pa_kernel(tc, h0, k1, k2, m1, m2, scaling, bia
         tile_last = {}
         for n in range(len(LOADS)):
             w, g, ja, jb, a, b = LOADS[n]
-            key = (w, g) if w == 0 else (w, a < HALF, g // 2)
+            key = (w, g)
             if key not in tile_order:
                 tile_order.append(key)
-            tile_last[key] = last_block(w, g, a, b)
+            tile_last[key] = last_block(w, g, 0, U)
             first = min(i for i, x in enumerate(BLOCKS) if x[0] == w and x[1] == g and a <= x[2] < b)
             step = max(first - 1 - (1 if jb < PACK else 0), -1)
             mult_at.setdefault(step, []).append(n)
@@ -155,7 +154,7 @@ def tile_sparsefactorisationdense_pa_kernel(tc, h0, k1, k2, m1, m2, scaling, bia
             while state["loaded"] < len(LOADS):
                 n = state["loaded"]
                 w, g, ja, jb, a, b = LOADS[n]
-                key = (w, g) if w == 0 else (w, a < HALF, g // 2)
+                key = (w, g)
                 if n >= state["mults"] + M_BUFS:
                     return
                 t = tile_order.index(key)
@@ -328,12 +327,12 @@ def tile_sparsefactorisationdense_pa_kernel(tc, h0, k1, k2, m1, m2, scaling, bia
                 h1_regroup(2)
                 h1_regroup(3)
                 h1_quant(0)
-            if s == LAST_A + 2:
-                for c in range(2):
-                    finish_gain(c)
-                    finish_relu(c)
-            if s == NB - 1:
-                finish_gain(2)
-                finish_relu(2)
-        finish_gain(3)
-        finish_relu(3)
+            if s >= 2:
+                w, g, a, b, sc = BLOCKS[s - 2]
+                if w == 1 and g == NG - 1:
+                    for c in range(a // CW, b // CW):
+                        finish_gain(c)
+                        finish_relu(c)
+        for c in range(BLOCKS[NB - 1][2] // CW, NC):
+            finish_gain(c)
+            finish_relu(c)

@@ -23,8 +23,7 @@ HALF = U // 2
 FLOPS = 2 * 2 * B * U * U
 
 BLOCKS = [
-    (0, 0, 0, 512, 384),
-    (0, 0, 512, 1024, 384),
+    (0, 0, 0, 1024, 832),
     (0, 0, 1024, 2048, 832),
     (0, 1, 0, 1024, 832),
     (0, 1, 1024, 2048, 832),
@@ -32,20 +31,19 @@ BLOCKS = [
     (0, 2, 1024, 2048, 832),
     (0, 3, 0, 1024, 832),
     (0, 3, 1024, 2048, 832),
-    (1, 0, 0, 1024, 640),
-    (1, 0, 1024, 2048, 640),
-    (1, 1, 0, 1024, 640),
-    (1, 1, 1024, 2048, 640),
-    (1, 2, 0, 1024, 768),
-    (1, 2, 1024, 2048, 768),
-    (1, 3, 0, 1024, 768),
+    (1, 0, 0, 1024, 576),
+    (1, 0, 1024, 2048, 576),
+    (1, 1, 0, 1024, 576),
+    (1, 1, 1024, 2048, 704),
+    (1, 2, 0, 1024, 704),
+    (1, 2, 1024, 2048, 704),
+    (1, 3, 0, 1024, 704),
     (1, 3, 1024, 1536, 384),
     (1, 3, 1536, 2048, 384),
 ]
 LOADS = [
-    (0, 0, 0, 4, 0, 512),
-    (0, 0, 0, 4, 512, 1024),
-    (0, 0, 0, 4, 1024, 2048),
+    (0, 0, 0, 2, 0, 2048),
+    (0, 0, 2, 4, 0, 2048),
     (0, 1, 0, 2, 0, 2048),
     (0, 1, 2, 4, 0, 2048),
     (0, 2, 0, 2, 0, 2048),
@@ -63,10 +61,17 @@ LOADS = [
     (1, 3, 0, 4, 1536, 2048),
 ]
 K_BUFS = 4
-M_BUFS = 6
-H0_AFTER = 3
-H0_STEP = 4
+M_BUFS = 5
+G_BUFS = 4
+C_BUFS = 6
+H0_AFTER = 2
+H0_STEP = 2
 BIAS_STEP = 1
+LEAD2 = 1
+LEAD = 1
+FIN = 1
+LAG = 1
+H1_STEP = 0
 FIRST2 = [x[0] for x in BLOCKS].index(1)
 
 
@@ -76,9 +81,9 @@ def tile_sparsefactorisationdense_pa_kernel(tc, h0, k1, k2, m1, m2, scaling, bia
         const = ctx.enter_context(tc.tile_pool(name="const", bufs=1))
         kpool = ctx.enter_context(tc.tile_pool(name="kpool", bufs=K_BUFS))
         mpool = ctx.enter_context(tc.tile_pool(name="mpool", bufs=M_BUFS))
-        grp = ctx.enter_context(tc.tile_pool(name="grp", bufs=3))
+        grp = ctx.enter_context(tc.tile_pool(name="grp", bufs=G_BUFS))
         hgp = ctx.enter_context(tc.tile_pool(name="hgp", bufs=1))
-        cod = ctx.enter_context(tc.tile_pool(name="cod", bufs=6))
+        cod = ctx.enter_context(tc.tile_pool(name="cod", bufs=C_BUFS))
         psum = ctx.enter_context(tc.psum_pool(name="psum", bufs=8))
         ctx.enter_context(tc.manual_schedule())
 
@@ -114,17 +119,17 @@ def tile_sparsefactorisationdense_pa_kernel(tc, h0, k1, k2, m1, m2, scaling, bia
             kt = ktiles[key]
             mt = mpool.tile([P, PACK * HALF], BF16, tag="m", name="mt%d" % n)
             e = (jb - ja) * (b - a)
-            if jb - ja < PACK:
+            if b - a == U:
                 lo = ja * U
-                src_views[(w, g)] = (kt[:].rearrange("p (j n) -> p j n", j=PACK), 0)
+                src_views.setdefault((w, g), []).append((0, U, kt[:].rearrange("p (j n) -> p j n", j=PACK)))
             else:
                 lo = PACK * a
                 view = kt[:, lo:lo + e].rearrange("p (j n) -> p j n", j=PACK)
-                src_views[(w, g, a)] = (view, a)
+                src_views.setdefault((w, g), []).append((a, b, view))
             kh = kt[:, lo:lo + e]
             mh = mt[:, 0:e]
-            for dst, src in ((kh, x), (mh, m)):
-                nc.sync.dma_start(out=dst.rearrange("p (j n) -> p j n", j=jb - ja),
+            for queue, dst, src in ((nc.sync, kh, x), (nc.sync, mh, m)):
+                queue.dma_start(out=dst.rearrange("p (j n) -> p j n", j=jb - ja),
                                   in_=src[rows, a:b].rearrange("(p j) n -> p j n", j=PACK)[:, ja:jb, :])
             mult_ops[n] = (kh, mh)
             if n == 0:
@@ -147,7 +152,7 @@ def tile_sparsefactorisationdense_pa_kernel(tc, h0, k1, k2, m1, m2, scaling, bia
                 tile_order.append(key)
             tile_last[key] = last_block(w, g, 0, U)
             first = min(i for i, x in enumerate(BLOCKS) if x[0] == w and x[1] == g and a <= x[2] < b)
-            step = max(first - 1 - (1 if jb < PACK else 0), -1)
+            step = max(first - (LEAD if w == 0 else LEAD2) - (1 if jb <= PACK // 2 else 0), -1)
             mult_at.setdefault(step, []).append(n)
 
         def pump_loads():
@@ -170,7 +175,7 @@ def tile_sparsefactorisationdense_pa_kernel(tc, h0, k1, k2, m1, m2, scaling, bia
 
         def regroup_part(n, engine_copy, lo, hi):
             w, g, a, b, sc = BLOCKS[n]
-            view, first = src_views[(w, g, a)] if (w, g, a) in src_views else src_views[(w, g)]
+            first, view = [(x[0], x[2]) for x in src_views[(w, g)] if x[0] <= a < x[1]][0]
             src = view[:, :, a - first:b - first]
             engine_copy(out=grouped[n][:, lo:hi, :].rearrange("p (c i) j -> p c j i", i=4),
                         in_=src[:, :, lo:hi].rearrange("p j (c i) -> p c j i", i=4))
@@ -271,22 +276,23 @@ def tile_sparsefactorisationdense_pa_kernel(tc, h0, k1, k2, m1, m2, scaling, bia
 
         bias_bc = const.tile([P, U], F32, name="bias_bc")
 
+        H1S = FIRST2 + H1_STEP
         pump_loads()
         pending = []
-        for s in range(NB + 1):
+        for s in range(NB + LAG):
             if s == 0:
                 for n in mult_at[-1]:
                     mult(n)
             if s < NB:
                 regroup_scalar(s)
-            if s >= 1:
-                quantise(s - 1)
+            if s >= LAG:
+                quantise(s - LAG)
             if s < NB:
                 regroup_vector(s)
             for n in mult_at.get(s, []):
                 mult(n)
-            if s >= 1:
-                pending.append(s - 1)
+            if s >= LAG:
+                pending.append(s - LAG)
             if s == BIAS_STEP:
                 pbs = []
                 for r in range(NC):
@@ -302,37 +308,38 @@ def tile_sparsefactorisationdense_pa_kernel(tc, h0, k1, k2, m1, m2, scaling, bia
                     evac_pass(xts[g], h0g[:].bitcast(F32), g)
             if s == H0_STEP + 1:
                 nc.vector.quantize_mx(out=h0c[:].bitcast(FP8X4), scales=h0s[:], in_=h0g[:])
-            if s == FIRST2 + 3:
+            if s == H1S + 3:
                 h1_quant(2)
             left = []
             for n in pending:
-                if BLOCKS[n][0] == 0 and s > H0_STEP or BLOCKS[n][0] == 1 and s >= FIRST2 + 3:
+                if BLOCKS[n][0] == 0 and s > H0_STEP or BLOCKS[n][0] == 1 and s >= H1S + 3:
                     matmuls(n)
                 else:
                     left.append(n)
             pending = left
-            if s == FIRST2:
+            if s == H1S:
                 h1_evac(0)
                 h1_evac(1)
                 h1_transpose(0)
                 h1_transpose(1)
-            if s == FIRST2 + 1:
+            if s == H1S + 1:
                 h1_evac(2)
                 h1_evac(3)
                 h1_transpose(2)
                 h1_transpose(3)
                 h1_regroup(0)
                 h1_regroup(1)
-            if s == FIRST2 + 2:
+            if s == H1S + 2:
                 h1_regroup(2)
                 h1_regroup(3)
                 h1_quant(0)
-            if s >= 2:
-                w, g, a, b, sc = BLOCKS[s - 2]
+            if s >= LAG + FIN:
+                w, g, a, b, sc = BLOCKS[s - LAG - FIN]
                 if w == 1 and g == NG - 1:
                     for c in range(a // CW, b // CW):
                         finish_gain(c)
                         finish_relu(c)
-        for c in range(BLOCKS[NB - 1][2] // CW, NC):
-            finish_gain(c)
-            finish_relu(c)
+        for n in range(NB - FIN, NB):
+            for c in range(BLOCKS[n][2] // CW, BLOCKS[n][3] // CW):
+                finish_gain(c)
+                finish_relu(c)

@@ -22,57 +22,16 @@ NC = U // CW
 HALF = U // 2
 FLOPS = 2 * 2 * B * U * U
 
-BLOCKS = [
-    (0, 0, 0, 1024, 832),
-    (0, 0, 1024, 2048, 832),
-    (0, 1, 0, 1024, 832),
-    (0, 1, 1024, 2048, 832),
-    (0, 2, 0, 1024, 832),
-    (0, 2, 1024, 2048, 832),
-    (0, 3, 0, 1024, 832),
-    (0, 3, 1024, 2048, 832),
-    (1, 0, 0, 1024, 576),
-    (1, 0, 1024, 2048, 576),
-    (1, 1, 0, 1024, 576),
-    (1, 1, 1024, 2048, 704),
-    (1, 2, 0, 1024, 704),
-    (1, 2, 1024, 2048, 704),
-    (1, 3, 0, 1024, 704),
-    (1, 3, 1024, 1536, 384),
-    (1, 3, 1536, 2048, 384),
-]
-LOADS = [
-    (0, 0, 0, 2, 0, 2048),
-    (0, 0, 2, 4, 0, 2048),
-    (0, 1, 0, 2, 0, 2048),
-    (0, 1, 2, 4, 0, 2048),
-    (0, 2, 0, 2, 0, 2048),
-    (0, 2, 2, 4, 0, 2048),
-    (0, 3, 0, 2, 0, 2048),
-    (0, 3, 2, 4, 0, 2048),
-    (1, 0, 0, 2, 0, 2048),
-    (1, 0, 2, 4, 0, 2048),
-    (1, 1, 0, 2, 0, 2048),
-    (1, 1, 2, 4, 0, 2048),
-    (1, 2, 0, 2, 0, 2048),
-    (1, 2, 2, 4, 0, 2048),
-    (1, 3, 0, 4, 0, 1024),
-    (1, 3, 0, 4, 1024, 1536),
-    (1, 3, 0, 4, 1536, 2048),
-]
+BLOCKS = ([(w, g, a, a + HALF) for w in range(2) for g in range(NG) for a in (0, HALF)][:-1]
+          + [(1, NG - 1, a, a + CW) for a in (HALF, HALF + CW)])
+NB = len(BLOCKS)
+FIRST2 = 2 * NG
+LAST_PASS = 2 * NG - 1
+SCALAR_COLS = (704, 640)
 K_BUFS = 4
-M_BUFS = 5
+M_BUFS = 6
 G_BUFS = 4
-C_BUFS = 6
-H0_AFTER = 2
-H0_STEP = 2
-BIAS_STEP = 1
-LEAD2 = 1
-LEAD = 1
-FIN = 1
-LAG = 1
-H1_STEP = 0
-FIRST2 = [x[0] for x in BLOCKS].index(1)
+CODE_BUFS = 6
 
 
 def tile_sparsefactorisationdense_pa_kernel(tc, h0, k1, k2, m1, m2, scaling, bias, out):
@@ -83,18 +42,9 @@ def tile_sparsefactorisationdense_pa_kernel(tc, h0, k1, k2, m1, m2, scaling, bia
         mpool = ctx.enter_context(tc.tile_pool(name="mpool", bufs=M_BUFS))
         grp = ctx.enter_context(tc.tile_pool(name="grp", bufs=G_BUFS))
         hgp = ctx.enter_context(tc.tile_pool(name="hgp", bufs=1))
-        cod = ctx.enter_context(tc.tile_pool(name="cod", bufs=C_BUFS))
+        cod = ctx.enter_context(tc.tile_pool(name="cod", bufs=CODE_BUFS))
         psum = ctx.enter_context(tc.psum_pool(name="psum", bufs=8))
         ctx.enter_context(tc.manual_schedule())
-
-        NB = len(BLOCKS)
-        ktiles = {}
-        src_views = {}
-        mult_ops = {}
-        mult_at = {}
-        grouped = {}
-        codes = {}
-        state = {"loaded": 0, "mults": 0, "regrouped": 0}
 
         brow = const.tile([P, U], BF16, name="brow")
         nc.vector.memset(brow[:], 0.0)
@@ -103,104 +53,99 @@ def tile_sparsefactorisationdense_pa_kernel(tc, h0, k1, k2, m1, m2, scaling, bia
         ident = const.tile([P, P], F32, name="ident")
         make_identity(nc, ident[:])
         warm = const.tile([P, P], BF16, name="warm")
-        nc.scalar.copy(out=warm[:], in_=ones[:])
-        sc_b = const.tile([P, 1], BF16, name="sc_b")
-        sc_f = const.tile([P, 1], F32, name="sc_f")
+        gain_b = const.tile([P, 1], BF16, name="gain_b")
+        gain = const.tile([P, 1], F32, name="gain")
+        bias_bc = const.tile([P, U], F32, name="bias_bc")
 
+        h0c = const.tile([P, NG * B], U32, name="h0c", align_bytes=64)
+        h0s = const.tile([P, NG * B], U8, name="h0s", align_bytes=64)
+        h1c = const.tile([P, NG * B], U32, name="h1c", align_bytes=64)
+        h1s = const.tile([P, NG * B], U8, name="h1s", align_bytes=64)
         h0_sb = hgp.tile([P, 2 * U], BF16, tag="hx", name="h0_sb")
+        h0g = hgp.tile([P, NG * B * PACK], BF16, tag="hg", name="h0g", align_bytes=64)
+
+        ktiles = {}
+        loads = []
+        for i in range(2 * NG):
+            if i < LAST_PASS:
+                loads.append((i // NG, i % NG, 0, 2, 0, U, 2 * i - 2))
+                loads.append((i // NG, i % NG, 2, PACK, 0, U, 2 * i - 1))
+        for n in range(2 * LAST_PASS, NB):
+            loads.append((1, NG - 1, 0, PACK, BLOCKS[n][2], BLOCKS[n][3], n - 1))
+        products = {}
+        done = {"loads": 0, "mults": 0, "regrouped": 0}
 
         def load(n):
-            w, g, ja, jb, a, b = LOADS[n]
-            x, m = (k1, m1) if w == 0 else (k2, m2)
-            rows = slice(g * KP, (g + 1) * KP)
-            key = (w, g)
-            if key not in ktiles:
-                ktiles[key] = kpool.tile([P, PACK * U], BF16, tag="k", name="kt%d" % n)
-            kt = ktiles[key]
-            mt = mpool.tile([P, PACK * HALF], BF16, tag="m", name="mt%d" % n)
-            e = (jb - ja) * (b - a)
-            if b - a == U:
-                lo = ja * U
-                src_views.setdefault((w, g), []).append((0, U, kt[:].rearrange("p (j n) -> p j n", j=PACK)))
-            else:
-                lo = PACK * a
-                view = kt[:, lo:lo + e].rearrange("p (j n) -> p j n", j=PACK)
-                src_views.setdefault((w, g), []).append((a, b, view))
-            kh = kt[:, lo:lo + e]
-            mh = mt[:, 0:e]
-            for queue, dst, src in ((nc.sync, kh, x), (nc.sync, mh, m)):
-                queue.dma_start(out=dst.rearrange("p (j n) -> p j n", j=jb - ja),
-                                  in_=src[rows, a:b].rearrange("(p j) n -> p j n", j=PACK)[:, ja:jb, :])
-            mult_ops[n] = (kh, mh)
+            w, g, ja, jb, a, b, step = loads[n]
+            if (w, g) not in ktiles:
+                ktiles[(w, g)] = kpool.tile([P, PACK * U], BF16, tag="k", name="k%d" % n)
+            mt = mpool.tile([P, PACK * HALF], BF16, tag="m", name="m%d" % n)
+            lo = ja * U if b - a == U else PACK * a
+            kh = ktiles[(w, g)][:, lo:lo + (jb - ja) * (b - a)]
+            mh = mt[:, 0:(jb - ja) * (b - a)]
+            for dst, src in ((kh, (k1, k2)[w]), (mh, (m1, m2)[w])):
+                rows = src[g * KP:(g + 1) * KP, a:b].rearrange("(p j) n -> p j n", j=PACK)
+                nc.sync.dma_start(out=dst.rearrange("p (j n) -> p j n", j=jb - ja), in_=rows[:, ja:jb, :])
+            products[n] = (kh, mh)
             if n == 0:
                 nc.sync.dma_start(out=brow[0:1, :], in_=bias.rearrange("(o n) -> o n", o=1))
-                nc.sync.dma_start(out=sc_b[:], in_=scaling.partition_broadcast(P))
-            if n + 1 == H0_AFTER:
+                nc.sync.dma_start(out=gain_b[:], in_=scaling.partition_broadcast(P))
+            if n == 1:
                 nc.sync.dma_start(out=h0_sb[:].rearrange("p (a k) -> p a k", a=2),
                                   in_=h0.rearrange("(a p) k -> p a k", p=P))
-            state["loaded"] = n + 1
-
-        def last_block(w, g, a, b):
-            return max(n for n, x in enumerate(BLOCKS) if x[0] == w and x[1] == g and a <= x[2] < b)
-
-        tile_order = []
-        tile_last = {}
-        for n in range(len(LOADS)):
-            w, g, ja, jb, a, b = LOADS[n]
-            key = (w, g)
-            if key not in tile_order:
-                tile_order.append(key)
-            tile_last[key] = last_block(w, g, 0, U)
-            first = min(i for i, x in enumerate(BLOCKS) if x[0] == w and x[1] == g and a <= x[2] < b)
-            step = max(first - (LEAD if w == 0 else LEAD2) - (1 if jb <= PACK // 2 else 0), -1)
-            mult_at.setdefault(step, []).append(n)
 
         def pump_loads():
-            while state["loaded"] < len(LOADS):
-                n = state["loaded"]
-                w, g, ja, jb, a, b = LOADS[n]
-                key = (w, g)
-                if n >= state["mults"] + M_BUFS:
-                    return
-                t = tile_order.index(key)
-                if key not in ktiles and t >= K_BUFS and tile_last[tile_order[t - K_BUFS]] >= state["regrouped"]:
+            while done["loads"] < len(loads) and done["loads"] < done["mults"] + M_BUFS:
+                n = done["loads"]
+                if 2 * (loads[n][0] * NG + loads[n][1] - K_BUFS + 1) > done["regrouped"]:
                     return
                 load(n)
+                done["loads"] = n + 1
 
-        def mult(n):
-            kh, mh = mult_ops[n]
-            nc.vector.tensor_tensor(out=kh, in0=kh, in1=mh, op=ALU.mult)
-            state["mults"] = n + 1
-            pump_loads()
+        def multiply(step):
+            for n in range(len(loads)):
+                if max(loads[n][6], -1) == step:
+                    kh, mh = products[n]
+                    nc.vector.tensor_tensor(out=kh, in0=kh, in1=mh, op=ALU.mult)
+                    done["mults"] = n + 1
+                    pump_loads()
+
+        grouped = {}
+
+        def scalar_cols(n):
+            w, g, a, b = BLOCKS[n]
+            return SCALAR_COLS[w] if b - a == HALF else 3 * (b - a) // 4
 
         def regroup_part(n, engine_copy, lo, hi):
-            w, g, a, b, sc = BLOCKS[n]
-            first, view = [(x[0], x[2]) for x in src_views[(w, g)] if x[0] <= a < x[1]][0]
-            src = view[:, :, a - first:b - first]
+            w, g, a, b = BLOCKS[n]
+            kt = ktiles[(w, g)]
+            if w * NG + g < LAST_PASS:
+                view = kt[:].rearrange("p (j n) -> p j n", j=PACK)[:, :, a:b]
+            else:
+                view = kt[:, PACK * a:PACK * b].rearrange("p (j n) -> p j n", j=PACK)
+            if n not in grouped:
+                grouped[n] = grp.tile([P, HALF, PACK], BF16, tag="g", name="g%d" % n, align_bytes=64)
             engine_copy(out=grouped[n][:, lo:hi, :].rearrange("p (c i) j -> p c j i", i=4),
-                        in_=src[:, :, lo:hi].rearrange("p j (c i) -> p c j i", i=4))
+                        in_=view[:, :, lo:hi].rearrange("p j (c i) -> p c j i", i=4))
 
         def regroup_scalar(n):
-            w, g, a, b, sc = BLOCKS[n]
-            grouped[n] = grp.tile([P, HALF, PACK], BF16, tag="g", name="gt%d" % n, align_bytes=64)
-            regroup_part(n, nc.scalar.copy, 0, sc)
+            regroup_part(n, nc.scalar.copy, 0, scalar_cols(n))
 
         def regroup_vector(n):
-            w, g, a, b, sc = BLOCKS[n]
-            if sc < b - a:
-                regroup_part(n, nc.vector.tensor_copy, sc, b - a)
-            state["regrouped"] = n + 1
-            pump_loads()
+            regroup_part(n, nc.vector.tensor_copy, scalar_cols(n), BLOCKS[n][3] - BLOCKS[n][2])
+
+        codes = {}
 
         def quantise(n):
-            w, g, a, b, sc = BLOCKS[n]
+            cols = BLOCKS[n][3] - BLOCKS[n][2]
             wc = cod.tile([P, HALF], U32, tag="wc", name="wc%d" % n, align_bytes=64)
             ws = cod.tile([P, HALF], U8, tag="ws", name="ws%d" % n, align_bytes=64)
             codes[n] = (wc, ws)
-            nc.vector.quantize_mx(out=wc[:, 0:b - a].bitcast(FP8X4), scales=ws[:, 0:b - a],
-                                  in_=grouped[n][:, 0:b - a, :].rearrange("p c j -> p (c j)"))
+            nc.vector.quantize_mx(out=wc[:, 0:cols].bitcast(FP8X4), scales=ws[:, 0:cols],
+                                  in_=grouped[n][:, 0:cols, :].rearrange("p c j -> p (c j)"))
 
-        def transpose_pass(words, g, name):
+        def transpose_pass(src, g, name):
+            words = src[:].bitcast(F32)
             xt = psum.tile([P, 2 * B], F32, tag="bank", name=name)
             for u in range(2):
                 for a in range(2):
@@ -209,137 +154,104 @@ def tile_sparsefactorisationdense_pa_kernel(tc, h0, k1, k2, m1, m2, scaling, bia
                                         words[:, base + u:base + KP // 2:2], ident[:])
             return xt
 
-        def evac_pass(xt, dst_words, g):
-            nc.scalar.copy(out=dst_words[:, g * 2 * B:(g + 1) * 2 * B].rearrange("p (b u) -> p b u", u=2),
+        def regroup_pass(xt, dst, g):
+            nc.scalar.copy(out=dst[:].bitcast(F32)[:, g * 2 * B:(g + 1) * 2 * B].rearrange("p (b u) -> p b u", u=2),
                            in_=xt[:].rearrange("p (u b) -> p b u", u=2))
 
-        h0c = const.tile([P, NG * B], U32, name="h0c", align_bytes=64)
-        h0s = const.tile([P, NG * B], U8, name="h0s", align_bytes=64)
-        h1c = const.tile([P, NG * B], U32, name="h1c", align_bytes=64)
-        h1s = const.tile([P, NG * B], U8, name="h1s", align_bytes=64)
-        h0g = hgp.tile([P, NG * B * PACK], BF16, tag="hg", name="h0g", align_bytes=64)
-
-        acc1 = {}
-        acc2 = {}
+        acc = {}
 
         def matmuls(n):
-            w, g, a0, b0, sc = BLOCKS[n]
-            lc, ls, acc = (h0c, h0s, acc1) if w == 0 else (h1c, h1s, acc2)
+            w, g, a, b = BLOCKS[n]
+            lc, ls = ((h0c, h0s), (h1c, h1s))[w]
             wc, ws = codes[n]
-            for c in range(a0 // CW, b0 // CW):
-                lo = c * CW - a0
-                for a in range(2):
+            for c in range(a // CW, b // CW):
+                for r in range(2):
                     if g == 0:
-                        acc[(a, c)] = psum.tile([P, CW], F32, tag="bank", name="acc%d_%d_%d" % (w, a, c))
-                    hl = g * B + a * P
+                        acc[(w, r, c)] = psum.tile([P, CW], F32, tag="bank", name="acc%d_%d_%d" % (w, r, c))
+                    hl = g * B + r * P
+                    lo = c * CW - a
                     nc.tensor.matmul_mx(
-                        out=acc[(a, c)][:],
+                        out=acc[(w, r, c)][:],
                         lhsT=lc[:, hl:hl + P].bitcast(FP8X4), lhsT_scale=ls[:, hl:hl + P],
                         rhs=wc[:, lo:lo + CW].bitcast(FP8X4), rhs_scale=ws[:, lo:lo + CW],
                         start=(g == 0), stop=(g == NG - 1))
 
-        late = {}
+        def store(n):
+            for c in range(BLOCKS[n][2] // CW, BLOCKS[n][3] // CW):
+                cols = slice(c * CW, (c + 1) * CW)
+                for r in range(2):
+                    nc.vector.scalar_tensor_tensor(out=o_sb[r][:, cols], in0=acc[(1, r, c)][:], scalar=gain[:, 0:1],
+                                                   in1=bias_bc[:, cols], op0=ALU.mult, op1=ALU.add)
+                for r in range(2):
+                    nc.scalar.activation(out=o_sb[r][:, cols], in_=o_sb[r][:, cols], func=ACT.Relu)
+                    nc.sync.dma_start(out=out[r * P:(r + 1) * P, cols], in_=o_sb[r][:, cols])
 
-        def h1_evac(c):
-            if c == 0:
-                late["h1"] = hgp.tile([P, 2 * U], BF16, tag="hx", name="h1_sb")
-            for a in range(2):
-                nc.scalar.copy(out=late["h1"][:, a * U + c * CW:a * U + (c + 1) * CW], in_=acc1[(a, c)][:])
-
-        def h1_transpose(g):
-            late["xt%d" % g] = transpose_pass(late["h1"][:].bitcast(F32), g, "yt%d" % g)
-
-        def h1_regroup(g):
-            if g == 0:
-                late["h1g"] = hgp.tile([P, NG * B * PACK], BF16, tag="hg", name="h1g", align_bytes=64)
-            evac_pass(late["xt%d" % g], late["h1g"][:].bitcast(F32), g)
-
-        def h1_quant(g0):
-            lo, hi = g0 * B, (g0 + 2) * B
-            nc.vector.quantize_mx(out=h1c[:, lo:hi].bitcast(FP8X4), scales=h1s[:, lo:hi],
-                                  in_=late["h1g"][:, lo * PACK:hi * PACK])
-
-        def finish_gain(c):
-            if c == 0:
-                late["o0"] = hgp.tile([P, U], F32, tag="hx", name="o0")
-                late["o1"] = hgp.tile([P, U], F32, tag="hg", name="o1", align_bytes=64)
-            for a in range(2):
-                nc.vector.scalar_tensor_tensor(out=late["o%d" % a][:, c * CW:(c + 1) * CW], in0=acc2[(a, c)][:],
-                                               scalar=sc_f[:, 0:1], in1=bias_bc[:, c * CW:(c + 1) * CW],
-                                               op0=ALU.mult, op1=ALU.add)
-
-        def finish_relu(c):
-            for a in range(2):
-                o = late["o%d" % a][:, c * CW:(c + 1) * CW]
-                nc.scalar.activation(out=o, in_=o, func=ACT.Relu)
-                nc.sync.dma_start(out=out[a * P:(a + 1) * P, c * CW:(c + 1) * CW], in_=o)
-
-        bias_bc = const.tile([P, U], F32, name="bias_bc")
-
-        H1S = FIRST2 + H1_STEP
         pump_loads()
-        pending = []
-        for s in range(NB + LAG):
-            if s == 0:
-                for n in mult_at[-1]:
-                    mult(n)
+        nc.scalar.copy(out=warm[:], in_=ones[:])
+        multiply(-1)
+        waiting = []
+        for s in range(NB + 1):
             if s < NB:
                 regroup_scalar(s)
-            if s >= LAG:
-                quantise(s - LAG)
+            if s == FIRST2:
+                h1g = hgp.tile([P, NG * B * PACK], BF16, tag="hg", name="h1g", align_bytes=64)
+            if s in (FIRST2, FIRST2 + 1):
+                for g in (2 * (s - FIRST2), 2 * (s - FIRST2) + 1):
+                    regroup_pass(h1t[g], h1g, g)
             if s < NB:
+                done["regrouped"] = s + 1
+                pump_loads()
+
+            for n in range(s - 1, s + 1):
+                if 0 <= n and (n == s - 1) != (n == FIRST2 - 1):
+                    quantise(n)
+                    waiting.append(n)
+            if s < 2 * LAST_PASS:
+                if s % 2 == 0:
+                    regroup_vector(s)
+                    regroup_vector(s + 1)
+            elif s < NB:
                 regroup_vector(s)
-            for n in mult_at.get(s, []):
-                mult(n)
-            if s >= LAG:
-                pending.append(s - LAG)
-            if s == BIAS_STEP:
-                pbs = []
-                for r in range(NC):
-                    pb = psum.tile([P, CW], F32, tag="bank", name="pb%d" % r)
-                    nc.tensor.matmul(out=pb[:], lhsT=ones[:], rhs=brow[:, r * CW:(r + 1) * CW], start=True, stop=True)
-                    pbs.append(pb)
-                for r in range(NC):
-                    nc.scalar.copy(out=bias_bc[:, r * CW:(r + 1) * CW], in_=pbs[r][:])
-                nc.vector.tensor_copy(out=sc_f[:], in_=sc_b[:])
-            if s == H0_STEP:
-                xts = [transpose_pass(h0_sb[:].bitcast(F32), g, "xt%d" % g) for g in range(NG)]
+
+            if s == 1:
+                pbs = [psum.tile([P, CW], F32, tag="bank", name="pb%d" % c) for c in range(NC)]
+                for c in range(NC):
+                    nc.tensor.matmul(out=pbs[c][:], lhsT=ones[:], rhs=brow[:, c * CW:(c + 1) * CW], start=True, stop=True)
+                for c in range(NC):
+                    nc.scalar.copy(out=bias_bc[:, c * CW:(c + 1) * CW], in_=pbs[c][:])
+                nc.vector.tensor_copy(out=gain[:], in_=gain_b[:])
+            if s == 2:
+                h0t = [transpose_pass(h0_sb, g, "h0t%d" % g) for g in range(NG)]
                 for g in range(NG):
-                    evac_pass(xts[g], h0g[:].bitcast(F32), g)
-            if s == H0_STEP + 1:
+                    regroup_pass(h0t[g], h0g, g)
+            if s == 3:
                 nc.vector.quantize_mx(out=h0c[:].bitcast(FP8X4), scales=h0s[:], in_=h0g[:])
-            if s == H1S + 3:
-                h1_quant(2)
+            if s in (FIRST2 + 1, FIRST2 + 2):
+                lo = 2 * (s - FIRST2 - 1) * B
+                hi = lo + 2 * B
+                nc.vector.quantize_mx(out=h1c[:, lo:hi].bitcast(FP8X4), scales=h1s[:, lo:hi],
+                                      in_=h1g[:, lo * PACK:hi * PACK])
+            multiply(s)
+
             left = []
-            for n in pending:
-                if BLOCKS[n][0] == 0 and s > H0_STEP or BLOCKS[n][0] == 1 and s >= H1S + 3:
+            for n in waiting:
+                if s >= (3 if n < FIRST2 else FIRST2 + 1 + BLOCKS[n][1] // 2):
                     matmuls(n)
                 else:
                     left.append(n)
-            pending = left
-            if s == H1S:
-                h1_evac(0)
-                h1_evac(1)
-                h1_transpose(0)
-                h1_transpose(1)
-            if s == H1S + 1:
-                h1_evac(2)
-                h1_evac(3)
-                h1_transpose(2)
-                h1_transpose(3)
-                h1_regroup(0)
-                h1_regroup(1)
-            if s == H1S + 2:
-                h1_regroup(2)
-                h1_regroup(3)
-                h1_quant(0)
-            if s >= LAG + FIN:
-                w, g, a, b, sc = BLOCKS[s - LAG - FIN]
-                if w == 1 and g == NG - 1:
-                    for c in range(a // CW, b // CW):
-                        finish_gain(c)
-                        finish_relu(c)
-        for n in range(NB - FIN, NB):
-            for c in range(BLOCKS[n][2] // CW, BLOCKS[n][3] // CW):
-                finish_gain(c)
-                finish_relu(c)
+            waiting = left
+
+            if s == FIRST2 - 1:
+                h1_sb = hgp.tile([P, 2 * U], BF16, tag="hx", name="h1_sb")
+                h1t = {}
+                for c in range(NC):
+                    for r in range(2):
+                        nc.scalar.copy(out=h1_sb[:, r * U + c * CW:r * U + (c + 1) * CW], in_=acc[(0, r, c)][:])
+                    h1t[c] = transpose_pass(h1_sb, c, "h1t%d" % c)
+
+            if s == 2 * LAST_PASS + 2:
+                o_sb = (hgp.tile([P, U], F32, tag="hx", name="o0"),
+                        hgp.tile([P, U], F32, tag="hg", name="o1", align_bytes=64))
+            if s >= 2 * LAST_PASS + 2:
+                store(s - 2)
+        store(NB - 1)

@@ -125,8 +125,8 @@ def tile_sparsefactorisationdense_pa_kernel(tc, h0, k1, k2, m1, m2, scaling, bia
                 view = kt[:, PACK * a:PACK * b].rearrange("p (j n) -> p j n", j=PACK)
             if n not in grouped:
                 grouped[n] = grp.tile([P, HALF, PACK], BF16, tag="g", name="g%d" % n, align_bytes=64)
-            engine_copy(out=grouped[n][:, lo:hi, :].rearrange("p (c i) j -> p c j i", i=4),
-                        in_=view[:, :, lo:hi].rearrange("p j (c i) -> p c j i", i=4))
+            engine_copy(out=grouped[n][:, lo:hi, :].rearrange("p (c i) j -> p c j i", i=8),
+                        in_=view[:, :, lo:hi].rearrange("p j (c i) -> p c j i", i=8))
 
         def regroup_scalar(n):
             regroup_part(n, nc.scalar.copy, 0, scalar_cols(n))

from contextlib import ExitStack

import concourse.mybir as mybir
from concourse.masks import make_identity

F32 = mybir.dt.float32
BF16 = mybir.dt.bfloat16
U32 = mybir.dt.uint32
U8 = mybir.dt.uint8
FP8X4 = mybir.dt.float8_e4m3fn_x4
ALU = mybir.AluOpType
ACT = mybir.ActivationFunctionType

P = 128
B = 256
U = 2048
PACK = 4
KP = P * PACK
NG = U // KP
CW = 512
NC = U // CW
HALF = U // 2
FLOPS = 2 * 2 * B * U * U

BLOCKS = ([(w, g, a, a + HALF) for w in range(2) for g in range(NG) for a in (0, HALF)][:-1]
          + [(1, NG - 1, a, a + CW) for a in (HALF, HALF + CW)])
NB = len(BLOCKS)
FIRST2 = 2 * NG
LAST_PASS = 2 * NG - 1
SCALAR_COLS = (704, 640)
K_BUFS = 4
M_BUFS = 6
G_BUFS = 4
CODE_BUFS = 6


def tile_sparsefactorisationdense_pa_kernel(tc, h0, k1, k2, m1, m2, scaling, bias, out):
    nc = tc.nc
    with ExitStack() as ctx:
        const = ctx.enter_context(tc.tile_pool(name="const", bufs=1))
        kpool = ctx.enter_context(tc.tile_pool(name="kpool", bufs=K_BUFS))
        mpool = ctx.enter_context(tc.tile_pool(name="mpool", bufs=M_BUFS))
        grp = ctx.enter_context(tc.tile_pool(name="grp", bufs=G_BUFS))
        hgp = ctx.enter_context(tc.tile_pool(name="hgp", bufs=1))
        cod = ctx.enter_context(tc.tile_pool(name="cod", bufs=CODE_BUFS))
        psum = ctx.enter_context(tc.psum_pool(name="psum", bufs=8))
        ctx.enter_context(tc.manual_schedule())

        brow = const.tile([P, U], BF16, name="brow")
        nc.vector.memset(brow[:], 0.0)
        ones = const.tile([P, P], BF16, name="ones")
        nc.vector.memset(ones[:], 1.0)
        ident = const.tile([P, P], F32, name="ident")
        make_identity(nc, ident[:])
        warm = const.tile([P, P], BF16, name="warm")
        gain_b = const.tile([P, 1], BF16, name="gain_b")
        gain = const.tile([P, 1], F32, name="gain")
        bias_bc = const.tile([P, U], F32, name="bias_bc")

        h0c = const.tile([P, NG * B], U32, name="h0c", align_bytes=64)
        h0s = const.tile([P, NG * B], U8, name="h0s", align_bytes=64)
        h1c = const.tile([P, NG * B], U32, name="h1c", align_bytes=64)
        h1s = const.tile([P, NG * B], U8, name="h1s", align_bytes=64)
        h0_sb = hgp.tile([P, 2 * U], BF16, tag="hx", name="h0_sb")
        h0g = hgp.tile([P, NG * B * PACK], BF16, tag="hg", name="h0g", align_bytes=64)

        ktiles = {}
        loads = []
        for i in range(2 * NG):
            if i < LAST_PASS:
                loads.append((i // NG, i % NG, 0, 2, 0, U, 2 * i - 2))
                loads.append((i // NG, i % NG, 2, PACK, 0, U, 2 * i - 1))
        for n in range(2 * LAST_PASS, NB):
            loads.append((1, NG - 1, 0, PACK, BLOCKS[n][2], BLOCKS[n][3], n - 1))
        products = {}
        done = {"loads": 0, "mults": 0, "regrouped": 0}

        def load(n):
            w, g, ja, jb, a, b, step = loads[n]
            if (w, g) not in ktiles:
                ktiles[(w, g)] = kpool.tile([P, PACK * U], BF16, tag="k", name="k%d" % n)
            mt = mpool.tile([P, PACK * HALF], BF16, tag="m", name="m%d" % n)
            lo = ja * U if b - a == U else PACK * a
            kh = ktiles[(w, g)][:, lo:lo + (jb - ja) * (b - a)]
            mh = mt[:, 0:(jb - ja) * (b - a)]
            for dst, src in ((kh, (k1, k2)[w]), (mh, (m1, m2)[w])):
                rows = src[g * KP:(g + 1) * KP, a:b].rearrange("(p j) n -> p j n", j=PACK)
                nc.sync.dma_start(out=dst.rearrange("p (j n) -> p j n", j=jb - ja), in_=rows[:, ja:jb, :])
            products[n] = (kh, mh)
            if n == 0:
                nc.sync.dma_start(out=brow[0:1, :], in_=bias.rearrange("(o n) -> o n", o=1))
                nc.sync.dma_start(out=gain_b[:], in_=scaling.partition_broadcast(P))
            if n == 1:
                nc.sync.dma_start(out=h0_sb[:].rearrange("p (a k) -> p a k", a=2),
                                  in_=h0.rearrange("(a p) k -> p a k", p=P))

        def pump_loads():
            while done["loads"] < len(loads) and done["loads"] < done["mults"] + M_BUFS:
                n = done["loads"]
                if 2 * (loads[n][0] * NG + loads[n][1] - K_BUFS + 1) > done["regrouped"]:
                    return
                load(n)
                done["loads"] = n + 1

        def multiply(step):
            for n in range(len(loads)):
                if max(loads[n][6], -1) == step:
                    kh, mh = products[n]
                    nc.vector.tensor_tensor(out=kh, in0=kh, in1=mh, op=ALU.mult)
                    done["mults"] = n + 1
                    pump_loads()

        grouped = {}

        def scalar_cols(n):
            w, g, a, b = BLOCKS[n]
            return SCALAR_COLS[w] if b - a == HALF else 3 * (b - a) // 4

        def regroup_part(n, engine_copy, lo, hi):
            w, g, a, b = BLOCKS[n]
            kt = ktiles[(w, g)]
            if w * NG + g < LAST_PASS:
                view = kt[:].rearrange("p (j n) -> p j n", j=PACK)[:, :, a:b]
            else:
                view = kt[:, PACK * a:PACK * b].rearrange("p (j n) -> p j n", j=PACK)
            if n not in grouped:
                grouped[n] = grp.tile([P, HALF, PACK], BF16, tag="g", name="g%d" % n, align_bytes=64)
            engine_copy(out=grouped[n][:, lo:hi, :].rearrange("p (c i) j -> p c j i", i=8),
                        in_=view[:, :, lo:hi].rearrange("p j (c i) -> p c j i", i=8))

        def regroup_scalar(n):
            regroup_part(n, nc.scalar.copy, 0, scalar_cols(n))

        def regroup_vector(n):
            regroup_part(n, nc.vector.tensor_copy, scalar_cols(n), BLOCKS[n][3] - BLOCKS[n][2])

        codes = {}

        def quantise(n):
            cols = BLOCKS[n][3] - BLOCKS[n][2]
            wc = cod.tile([P, HALF], U32, tag="wc", name="wc%d" % n, align_bytes=64)
            ws = cod.tile([P, HALF], U8, tag="ws", name="ws%d" % n, align_bytes=64)
            codes[n] = (wc, ws)
            nc.vector.quantize_mx(out=wc[:, 0:cols].bitcast(FP8X4), scales=ws[:, 0:cols],
                                  in_=grouped[n][:, 0:cols, :].rearrange("p c j -> p (c j)"))

        def transpose_pass(src, g, name):
            words = src[:].bitcast(F32)
            xt = psum.tile([P, 2 * B], F32, tag="bank", name=name)
            for u in range(2):
                for a in range(2):
                    base = a * (U // 2) + g * (KP // 2)
                    nc.tensor.transpose(xt[:, u * B + a * P:u * B + (a + 1) * P],
                                        words[:, base + u:base + KP // 2:2], ident[:])
            return xt

        def regroup_pass(xt, dst, g):
            nc.scalar.copy(out=dst[:].bitcast(F32)[:, g * 2 * B:(g + 1) * 2 * B].rearrange("p (b u) -> p b u", u=2),
                           in_=xt[:].rearrange("p (u b) -> p b u", u=2))

        acc = {}

        def matmuls(n):
            w, g, a, b = BLOCKS[n]
            lc, ls = ((h0c, h0s), (h1c, h1s))[w]
            wc, ws = codes[n]
            for c in range(a // CW, b // CW):
                for r in range(2):
                    if g == 0:
                        acc[(w, r, c)] = psum.tile([P, CW], F32, tag="bank", name="acc%d_%d_%d" % (w, r, c))
                    hl = g * B + r * P
                    lo = c * CW - a
                    nc.tensor.matmul_mx(
                        out=acc[(w, r, c)][:],
                        lhsT=lc[:, hl:hl + P].bitcast(FP8X4), lhsT_scale=ls[:, hl:hl + P],
                        rhs=wc[:, lo:lo + CW].bitcast(FP8X4), rhs_scale=ws[:, lo:lo + CW],
                        start=(g == 0), stop=(g == NG - 1))

        def store(n):
            for c in range(BLOCKS[n][2] // CW, BLOCKS[n][3] // CW):
                cols = slice(c * CW, (c + 1) * CW)
                for r in range(2):
                    nc.vector.scalar_tensor_tensor(out=o_sb[r][:, cols], in0=acc[(1, r, c)][:], scalar=gain[:, 0:1],
                                                   in1=bias_bc[:, cols], op0=ALU.mult, op1=ALU.add)
                for r in range(2):
                    nc.scalar.activation(out=o_sb[r][:, cols], in_=o_sb[r][:, cols], func=ACT.Relu)
                    nc.sync.dma_start(out=out[r * P:(r + 1) * P, cols], in_=o_sb[r][:, cols])

        pump_loads()
        nc.scalar.copy(out=warm[:], in_=ones[:])
        multiply(-1)
        waiting = []
        for s in range(NB + 1):
            if s < NB:
                regroup_scalar(s)
            if s == FIRST2:
                h1g = hgp.tile([P, NG * B * PACK], BF16, tag="hg", name="h1g", align_bytes=64)
            if s in (FIRST2, FIRST2 + 1):
                for g in (2 * (s - FIRST2), 2 * (s - FIRST2) + 1):
                    regroup_pass(h1t[g], h1g, g)
            if s < NB:
                done["regrouped"] = s + 1
                pump_loads()

            for n in range(s - 1, s + 1):
                if 0 <= n and (n == s - 1) != (n == FIRST2 - 1):
                    quantise(n)
                    waiting.append(n)
            if s < 2 * LAST_PASS:
                if s % 2 == 0:
                    regroup_vector(s)
                    regroup_vector(s + 1)
            elif s < NB:
                regroup_vector(s)

            if s == 1:
                pbs = [psum.tile([P, CW], F32, tag="bank", name="pb%d" % c) for c in range(NC)]
                for c in range(NC):
                    nc.tensor.matmul(out=pbs[c][:], lhsT=ones[:], rhs=brow[:, c * CW:(c + 1) * CW], start=True, stop=True)
                for c in range(NC):
                    nc.scalar.copy(out=bias_bc[:, c * CW:(c + 1) * CW], in_=pbs[c][:])
                nc.vector.tensor_copy(out=gain[:], in_=gain_b[:])
            if s == 2:
                h0t = [transpose_pass(h0_sb, g, "h0t%d" % g) for g in range(NG)]
                for g in range(NG):
                    regroup_pass(h0t[g], h0g, g)
            if s == 3:
                nc.vector.quantize_mx(out=h0c[:].bitcast(FP8X4), scales=h0s[:], in_=h0g[:])
            if s in (FIRST2 + 1, FIRST2 + 2):
                lo = 2 * (s - FIRST2 - 1) * B
                hi = lo + 2 * B
                nc.vector.quantize_mx(out=h1c[:, lo:hi].bitcast(FP8X4), scales=h1s[:, lo:hi],
                                      in_=h1g[:, lo * PACK:hi * PACK])
            multiply(s)

            left = []
            for n in waiting:
                if s >= (3 if n < FIRST2 else FIRST2 + 1 + BLOCKS[n][1] // 2):
                    matmuls(n)
                else:
                    left.append(n)
            waiting = left

            if s == FIRST2 - 1:
                h1_sb = hgp.tile([P, 2 * U], BF16, tag="hx", name="h1_sb")
                h1t = {}
                for c in range(NC):
                    for r in range(2):
                        nc.scalar.copy(out=h1_sb[:, r * U + c * CW:r * U + (c + 1) * CW], in_=acc[(0, r, c)][:])
                    h1t[c] = transpose_pass(h1_sb, c, "h1t%d" % c)

            if s == 2 * LAST_PASS + 2:
                o_sb = (hgp.tile([P, U], F32, tag="hx", name="o0"),
                        hgp.tile([P, U], F32, tag="hg", name="o1", align_bytes=64))
            if s >= 2 * LAST_PASS + 2:
                store(s - 2)
        store(NB - 1)
